import numpy as np
import ml_dtypes


def mxq(x, axis, fmt="e4m3"):
    dtype, down = {"e4m3": (ml_dtypes.float8_e4m3fn, 7), "e5m2": (ml_dtypes.float8_e5m2, 14)}[fmt]
    v = np.moveaxis(np.asarray(x, np.float32).astype(ml_dtypes.bfloat16).astype(np.float64), axis, -1)
    blocks = v.reshape(v.shape[:-1] + (-1, 32))
    amax = np.abs(blocks).max(-1, keepdims=True)
    byte = np.maximum(np.where(amax > 0, np.frexp(amax)[1] - 1 + 127, 0) - down, 1)
    scale = np.exp2(byte - 127.0)
    codes = (blocks / scale).astype(np.float32).astype(dtype).astype(np.float64)
    return np.moveaxis((codes * scale).reshape(v.shape), -1, axis)


WIDE = False


def mx_kscale(k):
    if not WIDE:
        return np.ones(k)
    levels = np.array([10, -10, 5, -5, 0])
    if k % 512:
        return np.exp2(np.random.permutation(np.resize(levels, k // 32))).repeat(32)
    a = np.empty((k // 512, 16))
    for p in range(k // 512):
        a[p, :8] = np.random.permutation(np.resize(levels, 8))
        for g in range(8):
            far = levels[np.abs(levels - a[p, g]) >= 10]
            a[p, g + 8] = far[np.random.randint(len(far))]
    return np.exp2(a.ravel()).repeat(32)


BF16 = ml_dtypes.bfloat16


def bf(x):
    return np.asarray(x, np.float32).astype(BF16)


def f64(x):
    return np.asarray(x).astype(np.float64)


B, S, D, H, QL, KL, ND, VD, RD = 4, 512, 8192, 16, 2048, 512, 128, 128, 128
QH = ND + RD
BASE = 10000.0


def rope(v):
    d = v.shape[-1]
    inv_freq = BASE ** (-np.arange(0, d, 2) / d)
    ang = np.arange(v.shape[1])[:, None] * inv_freq[None, :]
    cos = np.cos(ang)[None, :, None, :]
    sin = np.sin(ang)[None, :, None, :]
    v1 = v[..., 0::2]
    v2 = v[..., 1::2]
    o1 = v1 * cos - v2 * sin
    o2 = v1 * sin + v2 * cos
    return np.stack([o1, o2], axis=-1).reshape(v.shape)


def setup_inputs():
    s, t = mx_kscale(D), mx_kscale(QL)
    return {"x": bf(np.random.standard_normal((B, S, D)) * s),
            "Wqa": bf(np.random.standard_normal((D, QL)) / np.sqrt(D) / s[:, None] * t),
            "Wqb": bf(np.random.standard_normal((QL, H * QH)) / np.sqrt(QL) / t[:, None])}


def reference(x, Wqa, Wqb):
    cq = mxq(f64(x), 2, "e4m3") @ mxq(f64(Wqa), 0, "e4m3")
    q = (mxq(cq, 2, "e4m3") @ mxq(f64(Wqb), 0, "e4m3")).reshape(B, S, H, QH)
    q_nope, q_pe = q[..., :ND], q[..., ND:]
    return np.concatenate([q_nope, rope(q_pe)], axis=-1)

@@ -1,0 +1,563 @@
+from contextlib import ExitStack
+import math
+
+import concourse.masks as masks
+import concourse.mybir as mybir
+
+F32 = mybir.dt.float32
+BF16 = mybir.dt.bfloat16
+U32 = mybir.dt.uint32
+U8 = mybir.dt.uint8
+I32 = mybir.dt.int32
+FP8X4 = mybir.dt.float8_e4m3fn_x4
+ALU = mybir.AluOpType
+ACTF = mybir.ActivationFunctionType
+
+FLOPS = 2 * 2048 * 8192 * 2048 + 2 * 2048 * 2048 * 4096
+
+P = 128
+ROPE_BASE = 10000.0
+
+XC_OFF = 0
+XS_OFF = 131072
+U_OFF = 139264
+RAW_OFF = U_OFF
+XR_OFF = U_OFF + 8192
+WQ0_OFF = U_OFF + 16384
+GB_OFF = U_OFF + 32768
+CQ_OFF = U_OFF + 40960
+CQS_OFF = CQ_OFF + 24576
+WQ0S_OFF = CQS_OFF + 2048
+W0C_OFF = U_OFF + 45056
+W0S_OFF = U_OFF + 61440
+ID_OFF = U_OFF + 65536
+P_OFF = U_OFF + 68608
+WG_OFF = P_OFF
+RC_OFF = P_OFF + 4096
+RS_OFF = P_OFF + 10240
+CQ3_OFF = P_OFF
+CQ3S_OFF = P_OFF + 8192
+SL_OFF = P_OFF + 11776
+TB_OFF = SL_OFF + 16384
+QR_OFF = 0
+QG_OFF = 32768
+WQ_OFF = 40960
+WQ_SIZE = 17408
+OT_OFF = 93184
+T1_OFF = 117760
+T2_OFF = 123904
+
+SWEEPS = ((0, 1), (1, 0), (1, 1), (2, 0), (2, 1), (3, 0), (3, 1))
+LEAD = 4
+RING = 6
+
+
+def tile_multilatentattention_pa_l_kernel(tc, x, Wqa, Wqb, out):
+    nc = tc.nc
+    x2 = x.rearrange("b s d -> (b s) d")
+    out2 = out.rearrange("b s h d -> (b s) (h d)")
+
+    with ExitStack() as ctx:
+        sb = ctx.enter_context(tc.tile_pool(name="sb", bufs=1))
+        ps = ctx.enter_context(tc.psum_pool(name="ps", bufs=1))
+        ctx.enter_context(tc.manual_schedule())
+
+        def sbt(tag, shape, dtype, off):
+            return sb.tile(shape, dtype, name=tag, tag=tag, offset=off, align_bytes=64)
+
+        def bank(k):
+            return ps.tile([P, 512], F32, name="bank%d" % k, tag="bank%d" % k)
+
+        def copy(eng, dst, src):
+            if eng == "s":
+                nc.scalar.copy(out=dst, in_=src)
+            else:
+                nc.vector.tensor_copy(out=dst, in_=src)
+
+        def mx(acc, wc, wsc, mc, msc, start, stop):
+            nc.tensor.matmul_mx(
+                out=acc,
+                lhsT=wc.bitcast(FP8X4),
+                lhsT_scale=wsc,
+                rhs=mc.bitcast(FP8X4),
+                rhs_scale=msc,
+                start=start,
+                stop=stop,
+            )
+
+        cnt = {"wg": 0, "gb": 0, "ot": 0, "tt": 0}
+        xraw = {}
+        xgrp = {}
+        tpb = {}
+        xc = {}
+        xs = {}
+        w0 = {}
+        ring = {}
+        sl = {}
+        cq = {}
+        cqs = {}
+        cqg = {}
+        wq = {}
+        wqs = {}
+        acc = {}
+        tab = {}
+
+        def advance(st, target):
+            items = st["items"]
+            last = len(items) - 1
+            for k in range(st["q"], min(target, last) + 1):
+                for i in range(st["i"], min(k + 1, last) + 1):
+                    items[i]["inter"]()
+                    st["i"] = i + 1
+                prefetch(st, st["i"] - 1 + st["ahead"])
+                items[k]["quant"]()
+                st["q"] = k + 1
+
+        def prefetch(st, upto):
+            items = st["items"]
+            for d in range(st["d"], min(upto, len(items) - 1) + 1):
+                if items[d]["dma"] is not None:
+                    items[d]["dma"]()
+                st["d"] = d + 1
+
+        def w_item(c_chunk, h, g, idx, to_ring):
+            cell = {}
+
+            def dma():
+                if to_ring:
+                    rt = sbt("raw%d" % (idx % 4), [P, 4, 512], BF16, RAW_OFF + 4096 * (idx % 4))
+                else:
+                    rt = sbt("w0r%d" % g, [P, 4, 512], BF16, XC_OFF + 8192 * g + 4096)
+                nc.sync.dma_start(
+                    out=rt,
+                    in_=Wqa[512 * g : 512 * (g + 1), 512 * c_chunk : 512 * (c_chunk + 1)].rearrange(
+                        "(p j) c -> p j c", j=4
+                    ),
+                )
+                cell["raw"] = rt
+
+            def inter():
+                k = cnt["wg"] % 2
+                cnt["wg"] = cnt["wg"] + 1
+                wg = sbt("wg%d" % k, [P, 1024], BF16, WG_OFF + 2048 * k)
+                copy(
+                    "s" if idx % 2 == 0 else "v",
+                    wg.rearrange("p (t m j) -> p t m j", t=2, j=4),
+                    cell["raw"].rearrange("p j (m t) -> p t m j", t=4)[:, 2 * h : 2 * h + 2],
+                )
+                cell["wg"] = wg
+
+            def quant():
+                if to_ring:
+                    k = idx % RING
+                    codes = sbt("rc%d" % k, [P, 256], U32, RC_OFF + 1024 * k)
+                    scales = sbt("rs%d" % k, [P, 256], U8, RS_OFF + 256 * k)
+                    ring[idx] = (codes, scales)
+                else:
+                    codes = sbt("w0c%d" % g, [P, 256], U32, W0C_OFF + 1024 * g)
+                    scales = sbt("w0s%d" % g, [P, 256], U8, W0S_OFF + 256 * g)
+                    w0[g] = (codes, scales)
+                nc.vector.quantize_mx(out=codes.bitcast(FP8X4), scales=scales, in_=cell["wg"])
+
+            return {"dma": dma, "inter": inter, "quant": quant}
+
+        def q_load(grp, g2, hp, rt):
+            nc.sync.dma_start(
+                out=rt,
+                in_=Wqb[
+                    512 * g2 : 512 * (g2 + 1), 1024 * grp + 512 * hp : 1024 * grp + 512 * (hp + 1)
+                ].rearrange("(p j) c -> p j c", j=4),
+            )
+
+        def q_inter(eng, rt, kind, gt):
+            copy(
+                eng,
+                gt.rearrange("p (h c j) -> p h c j", h=2, j=4),
+                rt.rearrange("p j (h c) -> p h c j", h=2)[:, :, 128 * kind : 128 * (kind + 1), :],
+            )
+
+        def q_quant(grp, kind, g2, hp, gt):
+            base = WQ0_OFF if grp == 0 else WQ_OFF + WQ_SIZE * (grp - 1)
+            sbase = WQ0S_OFF if grp == 0 else base + 16384
+            if hp == 0:
+                wq[(grp, kind, g2)] = sbt(
+                    "wq%d_%d_%d" % (grp, kind, g2), [P, 512], U32, base + 2048 * (4 * kind + g2)
+                )
+                if g2 == 0:
+                    wqs[(grp, kind)] = sbt("wqs%d_%d" % (grp, kind), [P, 512], U8, sbase + 512 * kind)
+            nc.vector.quantize_mx(
+                out=wq[(grp, kind, g2)][:, 256 * hp : 256 * (hp + 1)].bitcast(FP8X4),
+                scales=wqs[(grp, kind)][4 * g2 : P, 256 * hp : 256 * (hp + 1)],
+                in_=gt,
+            )
+
+        def q_item(n, shared):
+            r, kind = divmod(n, 2)
+            grp = 1 + r // 8
+            g2, hp = divmod(r % 8, 2)
+            cell = {}
+
+            def dma():
+                rt = sbt("qr%d" % (r % 8), [P, 4, 512], BF16, QR_OFF + 4096 * (r % 8))
+                q_load(grp, g2, hp, rt)
+                shared[r] = rt
+
+            def inter():
+                gt = sbt("qg%d" % (n % 4), [P, 1024], BF16, QG_OFF + 2048 * (n % 4))
+                q_inter("s", shared[r], kind, gt)
+                cell["gt"] = gt
+
+            def quant():
+                q_quant(grp, kind, g2, hp, cell["gt"])
+
+            return {"dma": dma if kind == 0 else None, "inter": inter, "quant": quant}
+
+        w0s_stream = {"items": [w_item(0, 0, g, g, False) for g in range(16)], "d": 16, "i": 0, "q": 0, "ahead": 0}
+        ws = {
+            "items": [w_item(SWEEPS[q // 16][0], SWEEPS[q // 16][1], q % 16, q, True) for q in range(112)],
+            "d": 0,
+            "i": 0,
+            "q": 0,
+            "ahead": 0,
+        }
+        qshared = {}
+        qs = {"items": [q_item(n, qshared) for n in range(48)], "d": 0, "i": 0, "q": 0, "ahead": 14}
+
+        def tables_first():
+            ident = sbt("ident", [P, P], F32, ID_OFF)
+            masks.make_identity(nc, ident)
+            tab["ident"] = ident
+            pos_i = sbt("pos_i", [P, 4], I32, SL_OFF)
+            nc.gpsimd.iota(pos_i, pattern=[[128, 4]], base=0, channel_multiplier=1)
+            pos_f = sbt("pos_f", [P, 4], F32, SL_OFF + 64)
+            nc.vector.tensor_copy(out=pos_f, in_=pos_i)
+            turns = sbt("turns", [P, 2, 4, 64], F32, SL_OFF + 2048)
+            nc.gpsimd.tensor_scalar(
+                out=turns[:, 0, :, 0], in0=pos_f, scalar1=1.0 / (2.0 * math.pi), scalar2=None, op0=ALU.mult
+            )
+            for w in (1, 2, 4, 8, 16, 32):
+                nc.gpsimd.tensor_scalar(
+                    out=turns[:, 0, :, w : 2 * w],
+                    in0=turns[:, 0, :, 0:w],
+                    scalar1=ROPE_BASE ** (-w / 64.0),
+                    scalar2=None,
+                    op0=ALU.mult,
+                )
+            nc.gpsimd.tensor_scalar(out=turns[:, 1], in0=turns[:, 0], scalar1=0.25, scalar2=None, op0=ALU.add)
+            tab["turns"] = turns.rearrange("p s a j -> p (s a j)")
+
+        def tables_second():
+            turns = tab["turns"]
+            whole_i = sbt("whole_i", [P, 512], I32, SL_OFF + 4096)
+            nc.vector.tensor_copy(out=whole_i, in_=turns)
+            whole_f = sbt("whole_f", [P, 512], F32, SL_OFF + 6144)
+            nc.vector.tensor_copy(out=whole_f, in_=whole_i)
+            fr1 = sbt("fr1", [P, 512], F32, SL_OFF + 8192)
+            nc.vector.tensor_tensor(out=fr1, in0=turns, in1=whole_f, op=ALU.subtract)
+            fr2 = sbt("fr2", [P, 512], F32, SL_OFF + 10240)
+            nc.vector.scalar_tensor_tensor(out=fr2, in0=fr1, scalar=0.5, in1=fr1, op0=ALU.is_gt, op1=ALU.subtract)
+            fr3 = sbt("fr3", [P, 512], F32, SL_OFF + 12288)
+            nc.vector.scalar_tensor_tensor(out=fr3, in0=fr2, scalar=0.5, in1=fr2, op0=ALU.is_gt, op1=ALU.subtract)
+            tab["fr3"] = fr3
+
+        def tables_third():
+            tb = sbt("tb", [P, 3, 4, 64], F32, TB_OFF)
+            nc.scalar.activation(
+                out=tb[:, 0:2].rearrange("p s a j -> p (s a j)"), in_=tab["fr3"], func=ACTF.Sin, scale=2.0 * math.pi
+            )
+            tab["tb"] = tb
+
+        def tables_fourth():
+            tb = tab["tb"]
+            nc.vector.tensor_scalar(out=tb[:, 2], in0=tb[:, 0], scalar1=-1.0, scalar2=None, op0=ALU.mult)
+
+        def load_x(s):
+            b, rr = divmod(s, 8)
+            off = XR_OFF + 8192 * ((s + 1) % 3)
+            if s == 0:
+                xraw[s] = []
+                for i in range(4):
+                    t = sbt("xfirst%d" % i, [P, 1024], BF16, off + 2048 * i)
+                    nc.sync.dma_start(out=t, in_=x2[128 * i : 128 * (i + 1), 0:1024])
+                    xraw[s].append(t.bitcast(F32))
+            else:
+                t = sbt("xr%d" % (s % 3), [P, 4, 1024], BF16, off)
+                nc.sync.dma_start(
+                    out=t,
+                    in_=x2[512 * b : 512 * (b + 1), 1024 * rr : 1024 * (rr + 1)].rearrange("(i r) k -> r i k", r=P),
+                )
+                words = t.rearrange("r i k -> r (i k)").bitcast(F32)
+                xraw[s] = [words[:, 512 * i : 512 * (i + 1)] for i in range(4)]
+
+        def transposes(s):
+            for gl in range(2):
+                for ih in range(2):
+                    bk = bank(2 * gl + ih)
+                    tp = bk.rearrange("p (u r) -> p u r", u=2)
+                    tpb[(s, gl, ih)] = tp
+                    for il in range(2):
+                        for u in range(2):
+                            nc.tensor.transpose(
+                                out=tp[:, u, 128 * il : 128 * (il + 1)],
+                                in_=xraw[s][2 * ih + il][:, 256 * gl + u : 256 * (gl + 1) : 2],
+                                identity=tab["ident"],
+                            )
+
+        def copy_out(s):
+            for gl in range(2):
+                k = cnt["gb"] % 3
+                cnt["gb"] = cnt["gb"] + 1
+                xg = sbt("gb%d" % k, [P, 2048], BF16, GB_OFF + 4096 * k)
+                xgrp[(s, gl)] = xg
+                for ih in range(2):
+                    copy(
+                        "v" if (gl == 0 and ih == 0) else "s",
+                        xg.bitcast(F32)[:, 512 * ih : 512 * (ih + 1)].rearrange("p (r u) -> p r u", u=2),
+                        tpb[(s, gl, ih)].rearrange("p u r -> p r u"),
+                    )
+
+        def xplane(g, b):
+            return xs[(g // 4, b)][4 * (g % 4) : P, :]
+
+        def quant_x(s):
+            b, rr = divmod(s, 8)
+            for gl in range(2):
+                g = 2 * rr + gl
+                xc[(g, b)] = sbt("xc%d_%d" % (g, b), [P, 512], U32, XC_OFF + 2048 * (4 * g + b))
+                if g % 4 == 0:
+                    xs[(g // 4, b)] = sbt("xs%d_%d" % (g // 4, b), [P, 512], U8, XS_OFF + 512 * (g + b))
+                nc.vector.quantize_mx(out=xc[(g, b)].bitcast(FP8X4), scales=xplane(g, b), in_=xgrp[(s, gl)])
+
+        def mm_x(s):
+            b, rr = divmod(s, 8)
+            for gl in range(2):
+                g = 2 * rr + gl
+                for tau in range(2):
+                    if g == 0:
+                        acc[(b, tau)] = bank(4 + 2 * (b % 2) + tau)
+                    mx(
+                        acc[(b, tau)],
+                        w0[g][0][:, 128 * tau : 128 * (tau + 1)],
+                        w0[g][1][:, 128 * tau : 128 * (tau + 1)],
+                        xc[(g, b)],
+                        xplane(g, b),
+                        g == 0,
+                        g == 15,
+                    )
+            if rr == 7:
+                sl[b] = sbt("sl%d" % b, [P, 4, 512], BF16, SL_OFF + 4096 * b)
+                for tau in range(2):
+                    copy("s" if tau == 0 else "v", sl[b][:, tau, :], acc[(b, tau)])
+
+        def cq_inter(eng, b, gt):
+            copy(eng, gt.rearrange("p (n t) -> p n t", t=4), sl[b].rearrange("p t n -> p n t"))
+            cqg[b] = gt
+
+        def cq_quant(c_chunk, b):
+            if c_chunk < 3:
+                cq[(c_chunk, b)] = sbt("cq%d_%d" % (c_chunk, b), [P, 512], U32, CQ_OFF + 2048 * (4 * c_chunk + b))
+                if c_chunk == 0:
+                    tab[("cqsa", b)] = sbt("cqsa%d" % b, [P, 512], U8, CQS_OFF + 512 * b)
+                cqs[(c_chunk, b)] = tab[("cqsa", b)][4 * c_chunk : P, :]
+            else:
+                cq[(c_chunk, b)] = sbt("cq3_%d" % b, [P, 512], U32, CQ3_OFF + 2048 * b)
+                cqs[(c_chunk, b)] = sbt("cqsb%d" % b, [P, 512], U8, CQ3S_OFF + 512 * b)
+            nc.vector.quantize_mx(out=cq[(c_chunk, b)].bitcast(FP8X4), scales=cqs[(c_chunk, b)], in_=cqg[b])
+
+        def gb_tile():
+            k = cnt["gb"] % 2
+            cnt["gb"] = cnt["gb"] + 1
+            return sbt("gb%d" % k, [P, 2048], BF16, GB_OFF + 4096 * k)
+
+        tables_first()
+        for s in range(3):
+            load_x(s)
+            w0s_stream["items"][2 * s]["dma"]()
+            w0s_stream["items"][2 * s + 1]["dma"]()
+        for s in range(32):
+            transposes(s)
+            if s + 3 < 32:
+                load_x(s + 3)
+            if s + 3 < 8:
+                w0s_stream["items"][2 * (s + 3)]["dma"]()
+                w0s_stream["items"][2 * (s + 3) + 1]["dma"]()
+            if s >= 1:
+                quant_x(s - 1)
+            copy_out(s)
+            if s <= 8:
+                advance(w0s_stream, 2 * s - 1)
+            if s == 3:
+                tables_second()
+            if s == 5:
+                tables_third()
+            if s == 6:
+                tables_fourth()
+            if s == 27:
+                prefetch(ws, 1)
+            if s == 29:
+                advance(ws, 0)
+            if s == 30:
+                ws["ahead"] = 4
+                prefetch(ws, 5)
+            if s == 31:
+                advance(ws, 2)
+            if s >= 2:
+                mm_x(s - 2)
+        quant_x(31)
+        advance(ws, 4)
+
+        cnt["gb"] = 0
+        q0 = {}
+
+        def side_work(sw, g):
+            if sw in (1, 3, 5) and 1 <= g <= 8:
+                b, ph = divmod(g - 1, 2)
+                if ph == 0:
+                    cq_inter("v" if b % 2 == 0 else "s", b, gb_tile())
+                else:
+                    cq_quant(SWEEPS[sw - 1][0], b)
+            if g % 4 == 0 and q0.get("unit") is not None:
+                g2, hp = divmod(q0["unit"], 2)
+                for kind in range(2):
+                    q_quant(0, kind, g2, hp, q0[kind])
+                q0["unit"] = None
+            if sw in (2, 4):
+                k, ph = divmod(g, 4)
+                g2, hp = divmod(4 * (sw // 2 - 1) + k, 2)
+                if ph == 0:
+                    q0["raw"] = sbt("q0raw", [P, 4, 512], BF16, GB_OFF)
+                    q_load(0, g2, hp, q0["raw"])
+                if ph == 3:
+                    for kind in range(2):
+                        q0[kind] = sbt("q0g%d" % kind, [P, 1024], BF16, GB_OFF + 4096 + 2048 * kind)
+                        q_inter("s" if kind == 0 else "v", q0["raw"], kind, q0[kind])
+                    q0["unit"] = 4 * (sw // 2 - 1) + k
+            if sw == 6:
+                if g == 5:
+                    prefetch(qs, 15)
+                if g >= 8:
+                    advance(qs, g - 8)
+
+        def sweep_mm(sw, g, b):
+            h = SWEEPS[sw][1]
+            q = 16 * sw + g
+            for tau in range(2):
+                if g == 0:
+                    acc[(b, tau)] = bank(2 * b + tau)
+                mx(
+                    acc[(b, tau)],
+                    ring[q][0][:, 128 * tau : 128 * (tau + 1)],
+                    ring[q][1][:, 128 * tau : 128 * (tau + 1)],
+                    xc[(g, b)],
+                    xplane(g, b),
+                    g == 0,
+                    g == 15,
+                )
+                if g == 15:
+                    if h == 0 and tau == 0:
+                        sl[b] = sbt("sl%d" % b, [P, 4, 512], BF16, SL_OFF + 4096 * b)
+                    copy("s" if tau == 0 else "v", sl[b][:, 2 * h + tau, :], acc[(b, tau)])
+
+        for g in range(4):
+            sweep_mm(0, g, 2)
+        mm_x(30)
+        mm_x(31)
+        advance(ws, 5)
+        for b in (0, 1, 3):
+            for g in range(4):
+                sweep_mm(0, g, b)
+        for sw in range(7):
+            for g in range(4 if sw == 0 else 0, 16):
+                advance(ws, 16 * sw + g + LEAD)
+                side_work(sw, g)
+                for b in range(4):
+                    sweep_mm(sw, g, b)
+
+        def g3(b):
+            return sbt("g3_%d" % b, [P, 2048], BF16, OT_OFF + 4096 * b)
+
+        cq_inter("v", 0, g3(0))
+        cq_inter("s", 1, g3(1))
+        cq_quant(3, 0)
+        cq_inter("v", 2, g3(2))
+        cq_quant(3, 1)
+        cq_inter("s", 3, g3(3))
+        cq_quant(3, 2)
+        cq_quant(3, 3)
+
+        def s2_mm(grp, i, kind, bk, g2):
+            b, i4 = divmod(i, 4)
+            mx(
+                bk,
+                cq[(g2, b)][:, 128 * i4 : 128 * (i4 + 1)],
+                cqs[(g2, b)][:, 128 * i4 : 128 * (i4 + 1)],
+                wq[(grp, kind, g2)],
+                wqs[(grp, kind)][4 * g2 : P, :],
+                g2 == 0,
+                g2 == 3,
+            )
+
+        def finish(grp, i, bn, br, last):
+            a = i % 4
+            tb = tab["tb"]
+            k = cnt["ot"] % 6
+            cnt["ot"] = cnt["ot"] + 1
+            ot = sbt("ot%d" % k, [P, 4, 256], F32, OT_OFF + 4096 * k)
+            nc.scalar.copy(out=ot[:, :, 0:128], in_=bn.rearrange("p (h d) -> p h d", h=4))
+            k = cnt["tt"] % 3
+            cnt["tt"] = cnt["tt"] + 1
+            pr = br.rearrange("p (h j e) -> p h j e", h=4, e=2)
+            t1 = sbt("t1_%d" % k, [P, 4, 64, 2], F32, T1_OFF + 2048 * k)
+            t2 = sbt("t2_%d" % k, [P, 4, 2, 64], F32, T2_OFF + 2048 * k)
+            nc.vector.tensor_tensor(
+                out=t1, in0=pr, in1=tb[:, 1, a, :].unsqueeze(1).unsqueeze(3).to_broadcast([P, 4, 64, 2]), op=ALU.mult
+            )
+            nc.vector.tensor_tensor(
+                out=t2[:, :, 0, :],
+                in0=pr[:, :, :, 1],
+                in1=tb[:, 2, a, :].unsqueeze(1).to_broadcast([P, 4, 64]),
+                op=ALU.mult,
+            )
+            nc.vector.tensor_tensor(
+                out=t2[:, :, 1, :],
+                in0=pr[:, :, :, 0],
+                in1=tb[:, 0, a, :].unsqueeze(1).to_broadcast([P, 4, 64]),
+                op=ALU.mult,
+            )
+            adder = nc.vector if last else nc.gpsimd
+            adder.tensor_tensor(
+                out=ot[:, :, 128:256].rearrange("p h (j e) -> p h j e", e=2),
+                in0=t1,
+                in1=t2.rearrange("p h e j -> p h j e"),
+                op=ALU.add,
+            )
+            rows = out2[128 * i : 128 * (i + 1), 1024 * grp : 1024 * (grp + 1)]
+            if last:
+                for half in (1, 0):
+                    nc.sync.dma_start(
+                        out=rows.rearrange("p (h d) -> p h d", h=4)[:, :, 128 * half : 128 * (half + 1)],
+                        in_=ot[:, :, 128 * half : 128 * (half + 1)],
+                    )
+            else:
+                nc.sync.dma_start(out=rows, in_=ot.rearrange("p h d -> p (h d)"))
+
+        pre = {}
+        for i in range(4):
+            for kind in range(2):
+                pre[(i, kind)] = bank(2 * i + kind)
+                for g2 in range(3):
+                    s2_mm(0, i, kind, pre[(i, kind)], g2)
+        for i in range(4):
+            advance(qs, 8 + i)
+            for kind in range(2):
+                s2_mm(0, i, kind, pre[(i, kind)], 3)
+            finish(0, i, pre[(i, 0)], pre[(i, 1)], False)
+        for it in range(4, 64):
+            grp, i = divmod(it, 16)
+            advance(qs, 8 + it)
+            bn = bank((2 * i) % 8)
+            br = bank((2 * i + 1) % 8)
+            for kind in (1, 0) if it == 63 else (0, 1):
+                for g2 in range(4):
+                    s2_mm(grp, i, kind, br if kind == 1 else bn, g2)
+            finish(grp, i, bn, br, it == 63)

@@ -22,7 +22,9 @@ XC_OFF = 0
 XS_OFF = 131072
 U_OFF = 139264
 RAW_OFF = U_OFF
-XR_OFF = U_OFF + 8192
+XH_OFF = (U_OFF + 8192, U_OFF + 12288, U_OFF + 16384, U_OFF + 20480, U_OFF, U_OFF + 4096)
+SO_OFF = U_OFF + 24576
+SORT_FROM = 8
 WQ0_OFF = U_OFF + 16384
 GB_OFF = U_OFF + 32768
 CQ_OFF = U_OFF + 40960
@@ -85,13 +87,15 @@ def tile_multilatentattention_pa_l_kernel(tc, x, Wqa, Wqb, out):
                 stop=stop,
             )
 
-        cnt = {"wg": 0, "gb": 0, "ot": 0, "tt": 0}
+        cnt = {"gb": 0, "ot": 0, "tt": 0, "load": 0}
         xraw = {}
+        xsort = {}
         xgrp = {}
         tpb = {}
         xc = {}
         xs = {}
         w0 = {}
+        wraw = {}
         ring = {}
         sl = {}
         cq = {}
@@ -106,7 +110,7 @@ def tile_multilatentattention_pa_l_kernel(tc, x, Wqa, Wqb, out):
             items = st["items"]
             last = len(items) - 1
             for k in range(st["q"], min(target, last) + 1):
-                for i in range(st["i"], min(k + 1, last) + 1):
+                for i in range(st["i"], min(k + st["look"], last) + 1):
                     items[i]["inter"]()
                     st["i"] = i + 1
                 prefetch(st, st["i"] - 1 + st["ahead"])
@@ -120,46 +124,48 @@ def tile_multilatentattention_pa_l_kernel(tc, x, Wqa, Wqb, out):
                     items[d]["dma"]()
                 st["d"] = d + 1
 
-        def w_item(c_chunk, h, g, idx, to_ring):
+        def w_item(c_chunk, h, g, idx, first):
             cell = {}
 
             def dma():
-                if to_ring:
-                    rt = sbt("raw%d" % (idx % 4), [P, 4, 512], BF16, RAW_OFF + 4096 * (idx % 4))
-                else:
+                if first:
                     rt = sbt("w0r%d" % g, [P, 4, 512], BF16, XC_OFF + 8192 * g + 4096)
+                else:
+                    rt = sbt("raw%d" % (idx % 4), [P, 4, 512], BF16, RAW_OFF + 4096 * (idx % 4))
                 nc.sync.dma_start(
                     out=rt,
                     in_=Wqa[512 * g : 512 * (g + 1), 512 * c_chunk : 512 * (c_chunk + 1)].rearrange(
                         "(p j) c -> p j c", j=4
                     ),
                 )
-                cell["raw"] = rt
+                wraw[(first, g if first else idx)] = rt
 
             def inter():
-                k = cnt["wg"] % 2
-                cnt["wg"] = cnt["wg"] + 1
-                wg = sbt("wg%d" % k, [P, 1024], BF16, WG_OFF + 2048 * k)
+                k = idx % 4 if first else idx % 2
+                wg = sbt("wg%d" % k, [P, 1024], BF16, WG_OFF + 2048 * k if k < 2 else SL_OFF + 8192 + 2048 * k)
                 copy(
                     "s" if idx % 2 == 0 else "v",
                     wg.rearrange("p (t m j) -> p t m j", t=2, j=4),
-                    cell["raw"].rearrange("p j (m t) -> p t m j", t=4)[:, 2 * h : 2 * h + 2],
+                    wraw[(first, g if first else idx)].rearrange("p j (m t) -> p t m j", t=4)[:, 2 * h : 2 * h + 2],
                 )
                 cell["wg"] = wg
 
             def quant():
-                if to_ring:
-                    k = idx % RING
-                    codes = sbt("rc%d" % k, [P, 256], U32, RC_OFF + 1024 * k)
-                    scales = sbt("rs%d" % k, [P, 256], U8, RS_OFF + 256 * k)
-                    ring[idx] = (codes, scales)
-                else:
+                if first and h == 0:
                     codes = sbt("w0c%d" % g, [P, 256], U32, W0C_OFF + 1024 * g)
                     scales = sbt("w0s%d" % g, [P, 256], U8, W0S_OFF + 256 * g)
-                    w0[g] = (codes, scales)
+                    w0[(g, 0)] = (codes, scales)
+                else:
+                    k = g % RING if first else idx % RING
+                    codes = sbt("rc%d" % k, [P, 256], U32, RC_OFF + 1024 * k)
+                    scales = sbt("rs%d" % k, [P, 256], U8, RS_OFF + 256 * k)
+                    if first:
+                        w0[(g, 1)] = (codes, scales)
+                    else:
+                        ring[idx] = (codes, scales)
                 nc.vector.quantize_mx(out=codes.bitcast(FP8X4), scales=scales, in_=cell["wg"])
 
-            return {"dma": dma, "inter": inter, "quant": quant}
+            return {"dma": dma if (h == 0 or not first) else None, "inter": inter, "quant": quant}
 
         def q_load(grp, g2, hp, rt):
             nc.sync.dma_start(
@@ -204,7 +210,7 @@ def tile_multilatentattention_pa_l_kernel(tc, x, Wqa, Wqb, out):
 
             def inter():
                 gt = sbt("qg%d" % (n % 4), [P, 1024], BF16, QG_OFF + 2048 * (n % 4))
-                q_inter("s", shared[r], kind, gt)
+                q_inter("v" if (n < 16 and kind == 1) else "s", shared[r], kind, gt)
                 cell["gt"] = gt
 
             def quant():
@@ -212,16 +218,24 @@ def tile_multilatentattention_pa_l_kernel(tc, x, Wqa, Wqb, out):
 
             return {"dma": dma if kind == 0 else None, "inter": inter, "quant": quant}
 
-        w0s_stream = {"items": [w_item(0, 0, g, g, False) for g in range(16)], "d": 16, "i": 0, "q": 0, "ahead": 0}
+        w0s_stream = {
+            "items": [w_item(0, n % 2, n // 2, n, True) for n in range(32)],
+            "d": 32,
+            "i": 0,
+            "q": 0,
+            "ahead": 0,
+            "look": 2,
+        }
         ws = {
-            "items": [w_item(SWEEPS[q // 16][0], SWEEPS[q // 16][1], q % 16, q, True) for q in range(112)],
+            "items": [w_item(SWEEPS[q // 16][0], SWEEPS[q // 16][1], q % 16, q, False) for q in range(112)],
             "d": 0,
             "i": 0,
             "q": 0,
             "ahead": 0,
+            "look": 1,
         }
         qshared = {}
-        qs = {"items": [q_item(n, qshared) for n in range(48)], "d": 0, "i": 0, "q": 0, "ahead": 14}
+        qs = {"items": [q_item(n, qshared) for n in range(48)], "d": 0, "i": 0, "q": 0, "ahead": 14, "look": 1}
 
         def tables_first():
             ident = sbt("ident", [P, P], F32, ID_OFF)
@@ -254,9 +268,9 @@ def tile_multilatentattention_pa_l_kernel(tc, x, Wqa, Wqb, out):
             nc.vector.tensor_copy(out=whole_f, in_=whole_i)
             fr1 = sbt("fr1", [P, 512], F32, SL_OFF + 8192)
             nc.vector.tensor_tensor(out=fr1, in0=turns, in1=whole_f, op=ALU.subtract)
-            fr2 = sbt("fr2", [P, 512], F32, SL_OFF + 10240)
+            fr2 = sbt("fr2", [P, 512], F32, SL_OFF + 4096)
             nc.vector.scalar_tensor_tensor(out=fr2, in0=fr1, scalar=0.5, in1=fr1, op0=ALU.is_gt, op1=ALU.subtract)
-            fr3 = sbt("fr3", [P, 512], F32, SL_OFF + 12288)
+            fr3 = sbt("fr3", [P, 512], F32, SL_OFF + 6144)
             nc.vector.scalar_tensor_tensor(out=fr3, in0=fr2, scalar=0.5, in1=fr2, op0=ALU.is_gt, op1=ALU.subtract)
             tab["fr3"] = fr3
 
@@ -273,33 +287,62 @@ def tile_multilatentattention_pa_l_kernel(tc, x, Wqa, Wqb, out):
 
         def load_x(s):
             b, rr = divmod(s, 8)
-            off = XR_OFF + 8192 * ((s + 1) % 3)
-            if s == 0:
-                xraw[s] = []
-                for i in range(4):
-                    t = sbt("xfirst%d" % i, [P, 1024], BF16, off + 2048 * i)
-                    nc.sync.dma_start(out=t, in_=x2[128 * i : 128 * (i + 1), 0:1024])
-                    xraw[s].append(t.bitcast(F32))
-            else:
-                t = sbt("xr%d" % (s % 3), [P, 4, 1024], BF16, off)
-                nc.sync.dma_start(
-                    out=t,
-                    in_=x2[512 * b : 512 * (b + 1), 1024 * rr : 1024 * (rr + 1)].rearrange("(i r) k -> r i k", r=P),
+            xraw[s] = []
+            for half in range(2):
+                slot = (2 * s + half) % 6
+                row = 512 * b + 256 * half
+                if s == 0:
+                    for i in range(2):
+                        t = sbt("xfirst%d" % (2 * half + i), [P, 1024], BF16, XH_OFF[slot] + 2048 * i)
+                        nc.sync.dma_start(out=t, in_=x2[row + 128 * i : row + 128 * (i + 1), 0:1024])
+                        xraw[s].append(t.bitcast(F32))
+                else:
+                    t = sbt("xh%d" % slot, [P, 2, 1024], BF16, XH_OFF[slot])
+                    nc.sync.dma_start(
+                        out=t,
+                        in_=x2[row : row + 256, 1024 * rr : 1024 * (rr + 1)].rearrange("(i r) k -> r i k", r=P),
+                    )
+                    xraw[s].append(t.rearrange("r i k -> r (i k)").bitcast(F32))
+
+        def load_next():
+            s = cnt["load"]
+            if s < 32:
+                load_x(s)
+                if s < 8:
+                    w0s_stream["items"][4 * s]["dma"]()
+                    w0s_stream["items"][4 * s + 2]["dma"]()
+            cnt["load"] = s + 1
+
+        def sort_x(s):
+            xsort[s] = []
+            for half in range(2):
+                so = sbt("so%d" % half, [P, 1024], F32, SO_OFF + 4096 * half)
+                nc.vector.tensor_copy(
+                    out=so.rearrange("p (a u w) -> p a u w", a=4, u=2),
+                    in_=xraw[s][half].rearrange("p (a w u) -> p a u w", a=4, u=2),
                 )
-                words = t.rearrange("r i k -> r (i k)").bitcast(F32)
-                xraw[s] = [words[:, 512 * i : 512 * (i + 1)] for i in range(4)]
+                xsort[s].append(so)
+
+        def x_words(s, ih, il, gl, u):
+            if s >= SORT_FROM:
+                lo = 256 * (2 * il + gl) + 128 * u
+                return xsort[s][ih][:, lo : lo + 128]
+            if s == 0:
+                return xraw[s][2 * ih + il][:, 256 * gl + u : 256 * (gl + 1) : 2]
+            lo = 512 * il + 256 * gl
+            return xraw[s][ih][:, lo + u : lo + 256 : 2]
 
         def transposes(s):
-            for gl in range(2):
-                for ih in range(2):
-                    bk = bank(2 * gl + ih)
+            for ih in range(2):
+                for gl in range(2):
+                    bk = bank(2 * ih + gl)
                     tp = bk.rearrange("p (u r) -> p u r", u=2)
                     tpb[(s, gl, ih)] = tp
                     for il in range(2):
                         for u in range(2):
                             nc.tensor.transpose(
                                 out=tp[:, u, 128 * il : 128 * (il + 1)],
-                                in_=xraw[s][2 * ih + il][:, 256 * gl + u : 256 * (gl + 1) : 2],
+                                in_=x_words(s, ih, il, gl, u),
                                 identity=tab["ident"],
                             )
 
@@ -307,12 +350,12 @@ def tile_multilatentattention_pa_l_kernel(tc, x, Wqa, Wqb, out):
             for gl in range(2):
                 k = cnt["gb"] % 3
                 cnt["gb"] = cnt["gb"] + 1
-                xg = sbt("gb%d" % k, [P, 2048], BF16, GB_OFF + 4096 * k)
-                xgrp[(s, gl)] = xg
-                for ih in range(2):
+                xgrp[(s, gl)] = sbt("gb%d" % k, [P, 2048], BF16, GB_OFF + 4096 * k)
+            for ih in range(2):
+                for gl in range(2):
                     copy(
-                        "v" if (gl == 0 and ih == 0) else "s",
-                        xg.bitcast(F32)[:, 512 * ih : 512 * (ih + 1)].rearrange("p (r u) -> p r u", u=2),
+                        "v" if (s < SORT_FROM and gl == 0 and ih == 0) else "s",
+                        xgrp[(s, gl)].bitcast(F32)[:, 512 * ih : 512 * (ih + 1)].rearrange("p (r u) -> p r u", u=2),
                         tpb[(s, gl, ih)].rearrange("p u r -> p r u"),
                     )
 
@@ -332,13 +375,13 @@ def tile_multilatentattention_pa_l_kernel(tc, x, Wqa, Wqb, out):
             b, rr = divmod(s, 8)
             for gl in range(2):
                 g = 2 * rr + gl
-                for tau in range(2):
+                for t in range(4 if b == 0 else 2):
                     if g == 0:
-                        acc[(b, tau)] = bank(4 + 2 * (b % 2) + tau)
+                        acc[(b, t)] = bank(4 + (2 * (b % 2) + t) % 4)
                     mx(
-                        acc[(b, tau)],
-                        w0[g][0][:, 128 * tau : 128 * (tau + 1)],
-                        w0[g][1][:, 128 * tau : 128 * (tau + 1)],
+                        acc[(b, t)],
+                        w0[(g, t // 2)][0][:, 128 * (t % 2) : 128 * (t % 2 + 1)],
+                        w0[(g, t // 2)][1][:, 128 * (t % 2) : 128 * (t % 2 + 1)],
                         xc[(g, b)],
                         xplane(g, b),
                         g == 0,
@@ -346,8 +389,8 @@ def tile_multilatentattention_pa_l_kernel(tc, x, Wqa, Wqb, out):
                     )
             if rr == 7:
                 sl[b] = sbt("sl%d" % b, [P, 4, 512], BF16, SL_OFF + 4096 * b)
-                for tau in range(2):
-                    copy("s" if tau == 0 else "v", sl[b][:, tau, :], acc[(b, tau)])
+                for t in range(4 if b == 0 else 2):
+                    copy("s" if t % 2 == 0 else "v", sl[b][:, t, :], acc[(b, t)])
 
         def cq_inter(eng, b, gt):
             copy(eng, gt.rearrange("p (n t) -> p n t", t=4), sl[b].rearrange("p t n -> p n t"))
@@ -371,40 +414,41 @@ def tile_multilatentattention_pa_l_kernel(tc, x, Wqa, Wqb, out):
 
         tables_first()
         for s in range(3):
-            load_x(s)
-            w0s_stream["items"][2 * s]["dma"]()
-            w0s_stream["items"][2 * s + 1]["dma"]()
+            load_next()
         for s in range(32):
             transposes(s)
-            if s + 3 < 32:
-                load_x(s + 3)
-            if s + 3 < 8:
-                w0s_stream["items"][2 * (s + 3)]["dma"]()
-                w0s_stream["items"][2 * (s + 3) + 1]["dma"]()
             if s >= 1:
                 quant_x(s - 1)
+            if s < SORT_FROM:
+                load_next()
+            if SORT_FROM <= s + 1 < 32:
+                sort_x(s + 1)
+                load_next()
             copy_out(s)
             if s <= 8:
-                advance(w0s_stream, 2 * s - 1)
+                advance(w0s_stream, 4 * s - 1)
             if s == 3:
                 tables_second()
             if s == 5:
                 tables_third()
             if s == 6:
                 tables_fourth()
-            if s == 27:
+            if s == 28:
                 prefetch(ws, 1)
             if s == 29:
-                advance(ws, 0)
-            if s == 30:
+                prefetch(ws, 3)
                 ws["ahead"] = 4
-                prefetch(ws, 5)
+            if s == 30:
+                advance(ws, 0)
             if s == 31:
                 advance(ws, 2)
-            if s >= 2:
+            if 2 <= s <= 7:
                 mm_x(s - 2)
+            if s >= 9:
+                mm_x(s - 3)
         quant_x(31)
         advance(ws, 4)
+        mm_x(29)
 
         cnt["gb"] = 0
         q0 = {}
@@ -436,7 +480,7 @@ def tile_multilatentattention_pa_l_kernel(tc, x, Wqa, Wqb, out):
                 if g == 5:
                     prefetch(qs, 15)
                 if g >= 8:
-                    advance(qs, g - 8)
+                    advance(qs, 2 * (g - 8) + 1)
 
         def sweep_mm(sw, g, b):
             h = SWEEPS[sw][1]
@@ -463,14 +507,14 @@ def tile_multilatentattention_pa_l_kernel(tc, x, Wqa, Wqb, out):
         mm_x(30)
         mm_x(31)
         advance(ws, 5)
-        for b in (0, 1, 3):
+        for b in (1, 3):
             for g in range(4):
                 sweep_mm(0, g, b)
         for sw in range(7):
             for g in range(4 if sw == 0 else 0, 16):
                 advance(ws, 16 * sw + g + LEAD)
                 side_work(sw, g)
-                for b in range(4):
+                for b in range(1 if sw == 0 else 0, 4):
                     sweep_mm(sw, g, b)
 
         def g3(b):
@@ -548,13 +592,13 @@ def tile_multilatentattention_pa_l_kernel(tc, x, Wqa, Wqb, out):
                 for g2 in range(3):
                     s2_mm(0, i, kind, pre[(i, kind)], g2)
         for i in range(4):
-            advance(qs, 8 + i)
+            advance(qs, 16 + (4 * i) // 5)
             for kind in range(2):
                 s2_mm(0, i, kind, pre[(i, kind)], 3)
             finish(0, i, pre[(i, 0)], pre[(i, 1)], False)
         for it in range(4, 64):
             grp, i = divmod(it, 16)
-            advance(qs, 8 + it)
+            advance(qs, 16 + (4 * it) // 5)
             bn = bank((2 * i) % 8)
             br = bank((2 * i + 1) % 8)
             for kind in (1, 0) if it == 63 else (0, 1):

@@ -22,17 +22,17 @@ XC_OFF = 0
 XS_OFF = 131072
 U_OFF = 139264
 RAW_OFF = U_OFF
-XH_OFF = (U_OFF + 8192, U_OFF + 12288, U_OFF + 16384, U_OFF + 20480, U_OFF, U_OFF + 4096)
+XH_OFF = (U_OFF + 8192, U_OFF + 12288, U_OFF + 16384, U_OFF + 20480, U_OFF)
 SO_OFF = U_OFF + 24576
-SORT_FROM = 8
+SORT_FROM = 16
 WQ0_OFF = U_OFF + 16384
 GB_OFF = U_OFF + 32768
 CQ_OFF = U_OFF + 40960
 CQS_OFF = CQ_OFF + 24576
 WQ0S_OFF = CQS_OFF + 2048
 W0C_OFF = U_OFF + 45056
-W0S_OFF = U_OFF + 61440
-ID_OFF = U_OFF + 65536
+ID_OFF = U_OFF + 67584
+W0S_OFF = U_OFF + 68096
 P_OFF = U_OFF + 68608
 WG_OFF = P_OFF
 RC_OFF = P_OFF + 4096
@@ -41,6 +41,7 @@ CQ3_OFF = P_OFF
 CQ3S_OFF = P_OFF + 8192
 SL_OFF = P_OFF + 11776
 TB_OFF = SL_OFF + 16384
+EXT_OFF = TB_OFF + 3072
 QR_OFF = 0
 QG_OFF = 32768
 WQ_OFF = 40960
@@ -49,8 +50,9 @@ OT_OFF = 93184
 T1_OFF = 117760
 T2_OFF = 123904
 
-SWEEPS = ((0, 1), (1, 0), (1, 1), (2, 0), (2, 1), (3, 0), (3, 1))
+SWEEPS = ((1, 0), (1, 1), (2, 0), (2, 1), (3, 0), (3, 1))
 LEAD = 4
+W0_LEAD = 1
 RING = 6
 
 
@@ -110,12 +112,15 @@ def tile_multilatentattention_pa_l_kernel(tc, x, Wqa, Wqb, out):
             items = st["items"]
             last = len(items) - 1
             for k in range(st["q"], min(target, last) + 1):
+                for i in range(st["i"], k + 1):
+                    items[i]["inter"]()
+                    st["i"] = i + 1
+                items[k]["quant"]()
+                st["q"] = k + 1
                 for i in range(st["i"], min(k + st["look"], last) + 1):
                     items[i]["inter"]()
                     st["i"] = i + 1
                 prefetch(st, st["i"] - 1 + st["ahead"])
-                items[k]["quant"]()
-                st["q"] = k + 1
 
         def prefetch(st, upto):
             items = st["items"]
@@ -142,7 +147,7 @@ def tile_multilatentattention_pa_l_kernel(tc, x, Wqa, Wqb, out):
 
             def inter():
                 k = idx % 4 if first else idx % 2
-                wg = sbt("wg%d" % k, [P, 1024], BF16, WG_OFF + 2048 * k if k < 2 else SL_OFF + 8192 + 2048 * k)
+                wg = sbt("wg%d" % k, [P, 1024], BF16, WG_OFF + 2048 * k if k < 2 else SL_OFF + 4096 + 2048 * k)
                 copy(
                     "s" if idx % 2 == 0 else "v",
                     wg.rearrange("p (t m j) -> p t m j", t=2, j=4),
@@ -151,18 +156,31 @@ def tile_multilatentattention_pa_l_kernel(tc, x, Wqa, Wqb, out):
                 cell["wg"] = wg
 
             def quant():
-                if first and h == 0:
-                    codes = sbt("w0c%d" % g, [P, 256], U32, W0C_OFF + 1024 * g)
-                    scales = sbt("w0s%d" % g, [P, 256], U8, W0S_OFF + 256 * g)
-                    w0[(g, 0)] = (codes, scales)
+                if first:
+                    if idx < 6:
+                        off = RC_OFF + 1024 * idx
+                    elif idx < 28:
+                        off = W0C_OFF + 1024 * (idx - 6)
+                    elif idx < 31:
+                        off = TB_OFF + 1024 * (idx - 28)
+                    else:
+                        off = EXT_OFF
+                    codes = sbt("w0c%d" % idx, [P, 256], U32, off)
+                    if idx < 6:
+                        off = RS_OFF + 256 * idx
+                    elif idx < 22:
+                        off = SL_OFF + 12288 + 256 * (idx - 6)
+                    elif idx < 24:
+                        off = W0S_OFF + 256 * (idx - 22)
+                    else:
+                        off = EXT_OFF + 1024 + 256 * (idx - 24)
+                    scales = sbt("w0s%d" % idx, [P, 256], U8, off)
+                    w0[(g, h)] = (codes, scales)
                 else:
-                    k = g % RING if first else idx % RING
+                    k = idx % RING
                     codes = sbt("rc%d" % k, [P, 256], U32, RC_OFF + 1024 * k)
                     scales = sbt("rs%d" % k, [P, 256], U8, RS_OFF + 256 * k)
-                    if first:
-                        w0[(g, 1)] = (codes, scales)
-                    else:
-                        ring[idx] = (codes, scales)
+                    ring[idx] = (codes, scales)
                 nc.vector.quantize_mx(out=codes.bitcast(FP8X4), scales=scales, in_=cell["wg"])
 
             return {"dma": dma if (h == 0 or not first) else None, "inter": inter, "quant": quant}
@@ -227,7 +245,7 @@ def tile_multilatentattention_pa_l_kernel(tc, x, Wqa, Wqb, out):
             "look": 2,
         }
         ws = {
-            "items": [w_item(SWEEPS[q // 16][0], SWEEPS[q // 16][1], q % 16, q, False) for q in range(112)],
+            "items": [w_item(SWEEPS[q // 16][0], SWEEPS[q // 16][1], q % 16, q, False) for q in range(96)],
             "d": 0,
             "i": 0,
             "q": 0,
@@ -237,15 +255,17 @@ def tile_multilatentattention_pa_l_kernel(tc, x, Wqa, Wqb, out):
         qshared = {}
         qs = {"items": [q_item(n, qshared) for n in range(48)], "d": 0, "i": 0, "q": 0, "ahead": 14, "look": 1}
 
-        def tables_first():
+        def make_ident():
             ident = sbt("ident", [P, P], F32, ID_OFF)
             masks.make_identity(nc, ident)
             tab["ident"] = ident
-            pos_i = sbt("pos_i", [P, 4], I32, SL_OFF)
+
+        def tables_first():
+            pos_i = sbt("pos_i", [P, 4], I32, WQ0_OFF)
             nc.gpsimd.iota(pos_i, pattern=[[128, 4]], base=0, channel_multiplier=1)
-            pos_f = sbt("pos_f", [P, 4], F32, SL_OFF + 64)
+            pos_f = sbt("pos_f", [P, 4], F32, WQ0_OFF + 64)
             nc.vector.tensor_copy(out=pos_f, in_=pos_i)
-            turns = sbt("turns", [P, 2, 4, 64], F32, SL_OFF + 2048)
+            turns = sbt("turns", [P, 2, 4, 64], F32, WQ0_OFF + 2048)
             nc.gpsimd.tensor_scalar(
                 out=turns[:, 0, :, 0], in0=pos_f, scalar1=1.0 / (2.0 * math.pi), scalar2=None, op0=ALU.mult
             )
@@ -262,15 +282,15 @@ def tile_multilatentattention_pa_l_kernel(tc, x, Wqa, Wqb, out):
 
         def tables_second():
             turns = tab["turns"]
-            whole_i = sbt("whole_i", [P, 512], I32, SL_OFF + 4096)
+            whole_i = sbt("whole_i", [P, 512], I32, WQ0_OFF + 4096)
             nc.vector.tensor_copy(out=whole_i, in_=turns)
-            whole_f = sbt("whole_f", [P, 512], F32, SL_OFF + 6144)
+            whole_f = sbt("whole_f", [P, 512], F32, WQ0_OFF + 6144)
             nc.vector.tensor_copy(out=whole_f, in_=whole_i)
-            fr1 = sbt("fr1", [P, 512], F32, SL_OFF + 8192)
+            fr1 = sbt("fr1", [P, 512], F32, WQ0_OFF + 8192)
             nc.vector.tensor_tensor(out=fr1, in0=turns, in1=whole_f, op=ALU.subtract)
-            fr2 = sbt("fr2", [P, 512], F32, SL_OFF + 4096)
+            fr2 = sbt("fr2", [P, 512], F32, WQ0_OFF + 10240)
             nc.vector.scalar_tensor_tensor(out=fr2, in0=fr1, scalar=0.5, in1=fr1, op0=ALU.is_gt, op1=ALU.subtract)
-            fr3 = sbt("fr3", [P, 512], F32, SL_OFF + 6144)
+            fr3 = sbt("fr3", [P, 512], F32, WQ0_OFF + 12288)
             nc.vector.scalar_tensor_tensor(out=fr3, in0=fr2, scalar=0.5, in1=fr2, op0=ALU.is_gt, op1=ALU.subtract)
             tab["fr3"] = fr3
 
@@ -285,33 +305,29 @@ def tile_multilatentattention_pa_l_kernel(tc, x, Wqa, Wqb, out):
             tb = tab["tb"]
             nc.vector.tensor_scalar(out=tb[:, 2], in0=tb[:, 0], scalar1=-1.0, scalar2=None, op0=ALU.mult)
 
-        def load_x(s):
+        def load_half():
+            n = cnt["load"]
+            cnt["load"] = n + 1
+            if n >= 64:
+                return
+            s, half = divmod(n, 2)
             b, rr = divmod(s, 8)
-            xraw[s] = []
-            for half in range(2):
-                slot = (2 * s + half) % 6
-                row = 512 * b + 256 * half
-                if s == 0:
-                    for i in range(2):
-                        t = sbt("xfirst%d" % (2 * half + i), [P, 1024], BF16, XH_OFF[slot] + 2048 * i)
-                        nc.sync.dma_start(out=t, in_=x2[row + 128 * i : row + 128 * (i + 1), 0:1024])
-                        xraw[s].append(t.bitcast(F32))
-                else:
-                    t = sbt("xh%d" % slot, [P, 2, 1024], BF16, XH_OFF[slot])
-                    nc.sync.dma_start(
-                        out=t,
-                        in_=x2[row : row + 256, 1024 * rr : 1024 * (rr + 1)].rearrange("(i r) k -> r i k", r=P),
-                    )
-                    xraw[s].append(t.rearrange("r i k -> r (i k)").bitcast(F32))
-
-        def load_next():
-            s = cnt["load"]
-            if s < 32:
-                load_x(s)
-                if s < 8:
-                    w0s_stream["items"][4 * s]["dma"]()
-                    w0s_stream["items"][4 * s + 2]["dma"]()
-            cnt["load"] = s + 1
+            slot = n % 5
+            row = 512 * b + 256 * half
+            if half == 0:
+                xraw[s] = []
+            if s == 0:
+                for i in range(2):
+                    t = sbt("xfirst%d" % (2 * half + i), [P, 1024], BF16, XH_OFF[slot] + 2048 * i)
+                    nc.sync.dma_start(out=t, in_=x2[row + 128 * i : row + 128 * (i + 1), 0:1024])
+                    xraw[s].append(t.bitcast(F32))
+            else:
+                t = sbt("xh%d" % slot, [P, 2, 1024], BF16, XH_OFF[slot])
+                nc.sync.dma_start(
+                    out=t,
+                    in_=x2[row : row + 256, 1024 * rr : 1024 * (rr + 1)].rearrange("(i r) k -> r i k", r=P),
+                )
+                xraw[s].append(t.rearrange("r i k -> r (i k)").bitcast(F32))
 
         def sort_x(s):
             xsort[s] = []
@@ -322,6 +338,7 @@ def tile_multilatentattention_pa_l_kernel(tc, x, Wqa, Wqb, out):
                     in_=xraw[s][half].rearrange("p (a w u) -> p a u w", a=4, u=2),
                 )
                 xsort[s].append(so)
+                load_half()
 
         def x_words(s, ih, il, gl, u):
             if s >= SORT_FROM:
@@ -345,6 +362,11 @@ def tile_multilatentattention_pa_l_kernel(tc, x, Wqa, Wqb, out):
                                 in_=x_words(s, ih, il, gl, u),
                                 identity=tab["ident"],
                             )
+                if s < SORT_FROM and cnt["load"] < 32:
+                    load_half()
+                    if cnt["load"] == 32:
+                        for g in range(16):
+                            w0s_stream["items"][2 * g]["dma"]()
 
         def copy_out(s):
             for gl in range(2):
@@ -375,9 +397,9 @@ def tile_multilatentattention_pa_l_kernel(tc, x, Wqa, Wqb, out):
             b, rr = divmod(s, 8)
             for gl in range(2):
                 g = 2 * rr + gl
-                for t in range(4 if b == 0 else 2):
+                for t in range(4):
                     if g == 0:
-                        acc[(b, t)] = bank(4 + (2 * (b % 2) + t) % 4)
+                        acc[(b, t)] = bank(4 + t)
                     mx(
                         acc[(b, t)],
                         w0[(g, t // 2)][0][:, 128 * (t % 2) : 128 * (t % 2 + 1)],
@@ -389,7 +411,7 @@ def tile_multilatentattention_pa_l_kernel(tc, x, Wqa, Wqb, out):
                     )
             if rr == 7:
                 sl[b] = sbt("sl%d" % b, [P, 4, 512], BF16, SL_OFF + 4096 * b)
-                for t in range(4 if b == 0 else 2):
+                for t in range(4):
                     copy("s" if t % 2 == 0 else "v", sl[b][:, t, :], acc[(b, t)])
 
         def cq_inter(eng, b, gt):
@@ -412,75 +434,95 @@ def tile_multilatentattention_pa_l_kernel(tc, x, Wqa, Wqb, out):
             cnt["gb"] = cnt["gb"] + 1
             return sbt("gb%d" % k, [P, 2048], BF16, GB_OFF + 4096 * k)
 
-        tables_first()
-        for s in range(3):
-            load_next()
-        for s in range(32):
+        make_ident()
+        for n in range(5):
+            load_half()
+        for s in range(16):
             transposes(s)
             if s >= 1:
                 quant_x(s - 1)
-            if s < SORT_FROM:
-                load_next()
-            if SORT_FROM <= s + 1 < 32:
-                sort_x(s + 1)
-                load_next()
             copy_out(s)
-            if s <= 8:
-                advance(w0s_stream, 4 * s - 1)
-            if s == 3:
-                tables_second()
-            if s == 5:
-                tables_third()
-            if s == 6:
-                tables_fourth()
+        quant_x(15)
+        for g in range(16):
+            advance(w0s_stream, 2 * (g + W0_LEAD) + 1)
+            if g in (5, 7, 9, 11, 13):
+                load_half()
+            if g == 12:
+                sort_x(16)
+            for b in (1, 0) if g == 15 else (0, 1):
+                if g == 15:
+                    sl[b] = sbt("sl%d" % b, [P, 4, 512], BF16, SL_OFF + 4096 * b)
+                for t in range(4):
+                    if g == 0:
+                        acc[(b, t)] = bank(4 * (1 - b) + t)
+                    mx(
+                        acc[(b, t)],
+                        w0[(g, t // 2)][0][:, 128 * (t % 2) : 128 * (t % 2 + 1)],
+                        w0[(g, t // 2)][1][:, 128 * (t % 2) : 128 * (t % 2 + 1)],
+                        xc[(g, b)],
+                        xplane(g, b),
+                        g == 0,
+                        g == 15,
+                    )
+                    if g == 15:
+                        copy("s" if t % 2 == 0 else "v", sl[b][:, t, :], acc[(b, t)])
+        for s in range(16, 32):
+            transposes(s)
+            if s >= 17:
+                quant_x(s - 1)
+            if s + 1 < 32:
+                sort_x(s + 1)
+            copy_out(s)
             if s == 28:
                 prefetch(ws, 1)
             if s == 29:
                 prefetch(ws, 3)
                 ws["ahead"] = 4
-            if s == 30:
-                advance(ws, 0)
-            if s == 31:
-                advance(ws, 2)
-            if 2 <= s <= 7:
-                mm_x(s - 2)
-            if s >= 9:
+            if s >= 19:
                 mm_x(s - 3)
         quant_x(31)
         advance(ws, 4)
         mm_x(29)
+        mm_x(30)
+        mm_x(31)
 
         cnt["gb"] = 0
         q0 = {}
 
         def side_work(sw, g):
-            if sw in (1, 3, 5) and 1 <= g <= 8:
-                b, ph = divmod(g - 1, 2)
+            if sw in (0, 2, 4) and 3 <= g <= 10:
+                b, ph = divmod(g - 3, 2)
                 if ph == 0:
                     cq_inter("v" if b % 2 == 0 else "s", b, gb_tile())
                 else:
-                    cq_quant(SWEEPS[sw - 1][0], b)
-            if g % 4 == 0 and q0.get("unit") is not None:
-                g2, hp = divmod(q0["unit"], 2)
-                for kind in range(2):
-                    q_quant(0, kind, g2, hp, q0[kind])
-                q0["unit"] = None
-            if sw in (2, 4):
-                k, ph = divmod(g, 4)
-                g2, hp = divmod(4 * (sw // 2 - 1) + k, 2)
-                if ph == 0:
-                    q0["raw"] = sbt("q0raw", [P, 4, 512], BF16, GB_OFF)
-                    q_load(0, g2, hp, q0["raw"])
-                if ph == 3:
-                    for kind in range(2):
-                        q0[kind] = sbt("q0g%d" % kind, [P, 1024], BF16, GB_OFF + 4096 + 2048 * kind)
-                        q_inter("s" if kind == 0 else "v", q0["raw"], kind, q0[kind])
-                    q0["unit"] = 4 * (sw // 2 - 1) + k
-            if sw == 6:
-                if g == 5:
-                    prefetch(qs, 15)
+                    cq_quant(sw // 2, b)
+            if sw == 0:
+                if g == 1:
+                    tables_first()
+                if g == 11:
+                    tables_second()
+                if g == 13:
+                    tables_third()
+                if g == 14:
+                    tables_fourth()
+            for j in range(2):
+                for k in range(4):
+                    g2, hp = divmod(4 * j + k, 2)
+                    if (sw, g) == (2 * j + 1, 4 * k):
+                        q0["raw"] = sbt("q0raw", [P, 4, 512], BF16, GB_OFF)
+                        q_load(0, g2, hp, q0["raw"])
+                    if (sw, g) == ((2 * j + 1, 4 * k + 3) if k < 3 else (2 * j + 2, 0)):
+                        for kind in range(2):
+                            q0[kind] = sbt("q0g%d" % kind, [P, 1024], BF16, GB_OFF + 4096 + 2048 * kind)
+                            q_inter("s" if kind == 0 else "v", q0["raw"], kind, q0[kind])
+                    if (sw, g) == ((2 * j + 1, 4 * k + 4) if k < 3 else (2 * j + 2, 2)):
+                        for kind in range(2):
+                            q_quant(0, kind, g2, hp, q0[kind])
+            if sw == 5:
                 if g >= 8:
-                    advance(qs, 2 * (g - 8) + 1)
+                    prefetch(qs, min(15, 4 * (g - 7) - 1))
+                if g >= 11:
+                    advance(qs, 2 * (g - 11) + 1)
 
         def sweep_mm(sw, g, b):
             h = SWEEPS[sw][1]
@@ -502,19 +544,11 @@ def tile_multilatentattention_pa_l_kernel(tc, x, Wqa, Wqb, out):
                         sl[b] = sbt("sl%d" % b, [P, 4, 512], BF16, SL_OFF + 4096 * b)
                     copy("s" if tau == 0 else "v", sl[b][:, 2 * h + tau, :], acc[(b, tau)])
 
-        for g in range(4):
-            sweep_mm(0, g, 2)
-        mm_x(30)
-        mm_x(31)
-        advance(ws, 5)
-        for b in (1, 3):
-            for g in range(4):
-                sweep_mm(0, g, b)
-        for sw in range(7):
-            for g in range(4 if sw == 0 else 0, 16):
+        for sw in range(6):
+            for g in range(16):
                 advance(ws, 16 * sw + g + LEAD)
                 side_work(sw, g)
-                for b in range(1 if sw == 0 else 0, 4):
+                for b in range(4):
                     sweep_mm(sw, g, b)
 
         def g3(b):
@@ -592,13 +626,13 @@ def tile_multilatentattention_pa_l_kernel(tc, x, Wqa, Wqb, out):
                 for g2 in range(3):
                     s2_mm(0, i, kind, pre[(i, kind)], g2)
         for i in range(4):
-            advance(qs, 16 + (4 * i) // 5)
+            advance(qs, 10 + i)
             for kind in range(2):
                 s2_mm(0, i, kind, pre[(i, kind)], 3)
             finish(0, i, pre[(i, 0)], pre[(i, 1)], False)
         for it in range(4, 64):
             grp, i = divmod(it, 16)
-            advance(qs, 16 + (4 * it) // 5)
+            advance(qs, 10 + (7 * it) // 8 if it > 8 else 10 + it)
             bn = bank((2 * i) % 8)
             br = bank((2 * i + 1) % 8)
             for kind in (1, 0) if it == 63 else (0, 1):

@@ -53,6 +53,7 @@ T2_OFF = 123904
 SWEEPS = ((1, 0), (1, 1), (2, 0), (2, 1), (3, 0), (3, 1))
 LEAD = 4
 W0_LEAD = 1
+HELD_FROM = 13
 RING = 6
 
 
@@ -89,7 +90,7 @@ def tile_multilatentattention_pa_l_kernel(tc, x, Wqa, Wqb, out):
                 stop=stop,
             )
 
-        cnt = {"gb": 0, "ot": 0, "tt": 0, "load": 0}
+        cnt = {"gb": 0, "ot": 0, "tt": 0, "load": 32}
         xraw = {}
         xsort = {}
         xgrp = {}
@@ -316,18 +317,12 @@ def tile_multilatentattention_pa_l_kernel(tc, x, Wqa, Wqb, out):
             row = 512 * b + 256 * half
             if half == 0:
                 xraw[s] = []
-            if s == 0:
-                for i in range(2):
-                    t = sbt("xfirst%d" % (2 * half + i), [P, 1024], BF16, XH_OFF[slot] + 2048 * i)
-                    nc.sync.dma_start(out=t, in_=x2[row + 128 * i : row + 128 * (i + 1), 0:1024])
-                    xraw[s].append(t.bitcast(F32))
-            else:
-                t = sbt("xh%d" % slot, [P, 2, 1024], BF16, XH_OFF[slot])
-                nc.sync.dma_start(
-                    out=t,
-                    in_=x2[row : row + 256, 1024 * rr : 1024 * (rr + 1)].rearrange("(i r) k -> r i k", r=P),
-                )
-                xraw[s].append(t.rearrange("r i k -> r (i k)").bitcast(F32))
+            t = sbt("xh%d" % slot, [P, 2, 1024], BF16, XH_OFF[slot])
+            nc.sync.dma_start(
+                out=t,
+                in_=x2[row : row + 256, 1024 * rr : 1024 * (rr + 1)].rearrange("(i r) k -> r i k", r=P),
+            )
+            xraw[s].append(t.rearrange("r i k -> r (i k)").bitcast(F32))
 
         def sort_x(s):
             xsort[s] = []
@@ -341,13 +336,8 @@ def tile_multilatentattention_pa_l_kernel(tc, x, Wqa, Wqb, out):
                 load_half()
 
         def x_words(s, ih, il, gl, u):
-            if s >= SORT_FROM:
-                lo = 256 * (2 * il + gl) + 128 * u
-                return xsort[s][ih][:, lo : lo + 128]
-            if s == 0:
-                return xraw[s][2 * ih + il][:, 256 * gl + u : 256 * (gl + 1) : 2]
-            lo = 512 * il + 256 * gl
-            return xraw[s][ih][:, lo + u : lo + 256 : 2]
+            lo = 256 * (2 * il + gl) + 128 * u
+            return xsort[s][ih][:, lo : lo + 128]
 
         def transposes(s):
             for ih in range(2):
@@ -362,11 +352,6 @@ def tile_multilatentattention_pa_l_kernel(tc, x, Wqa, Wqb, out):
                                 in_=x_words(s, ih, il, gl, u),
                                 identity=tab["ident"],
                             )
-                if s < SORT_FROM and cnt["load"] < 32:
-                    load_half()
-                    if cnt["load"] == 32:
-                        for g in range(16):
-                            w0s_stream["items"][2 * g]["dma"]()
 
         def copy_out(s):
             for gl in range(2):
@@ -376,10 +361,68 @@ def tile_multilatentattention_pa_l_kernel(tc, x, Wqa, Wqb, out):
             for ih in range(2):
                 for gl in range(2):
                     copy(
-                        "v" if (s < SORT_FROM and gl == 0 and ih == 0) else "s",
+                        "s",
                         xgrp[(s, gl)].bitcast(F32)[:, 512 * ih : 512 * (ih + 1)].rearrange("p (r u) -> p r u", u=2),
                         tpb[(s, gl, ih)].rearrange("p u r -> p r u"),
                     )
+
+        def load_a(s):
+            b, rest = divmod(s, 8)
+            kh, i4 = divmod(rest, 4)
+            row = 512 * b + 128 * i4
+            off = U_OFF + 8192 * (s % 4)
+            if s == 0:
+                xraw[s] = []
+                for j in range(4):
+                    t = sbt("xfirst%d" % j, [P, 1024], BF16, off + 2048 * j)
+                    nc.sync.dma_start(out=t, in_=x2[row : row + 128, 1024 * j : 1024 * (j + 1)])
+                    xraw[s].append(t.bitcast(F32))
+            else:
+                t = sbt("xa%d" % (s % 4), [P, 4096], BF16, off)
+                nc.sync.dma_start(out=t, in_=x2[row : row + 128, 4096 * kh : 4096 * (kh + 1)])
+                words = t.bitcast(F32)
+                xraw[s] = [words[:, 512 * j : 512 * (j + 1)] for j in range(4)]
+
+        def transposes_a(s):
+            for j in range(4):
+                tp = bank(j).rearrange("p (g u r) -> p g u r", g=2, u=2)
+                tpb[(s, j)] = tp
+                for gl in range(2):
+                    for u in range(2):
+                        nc.tensor.transpose(
+                            out=tp[:, gl, u, :],
+                            in_=xraw[s][j][:, 256 * gl + u : 256 * (gl + 1) : 2],
+                            identity=tab["ident"],
+                        )
+
+        def copy_out_a(s):
+            for jj in range(2):
+                k = cnt["gb"] % 3
+                cnt["gb"] = cnt["gb"] + 1
+                xgrp[(s, jj)] = sbt("gb%d" % k, [P, 2048], BF16, GB_OFF + 4096 * k)
+                for jl in range(2):
+                    copy(
+                        "v" if (jj == 0 and jl == 0) else "s",
+                        xgrp[(s, jj)].bitcast(F32)[:, 512 * jl : 512 * (jl + 1)].rearrange(
+                            "p (g r u) -> p g r u", g=2, u=2
+                        ),
+                        tpb[(s, 2 * jj + jl)].rearrange("p g u r -> p g r u"),
+                    )
+
+        def quant_a(s):
+            b, rest = divmod(s, 8)
+            kh, i4 = divmod(rest, 4)
+            for q in range(8):
+                g = 8 * kh + q
+                if i4 == 0:
+                    xc[(g, b)] = sbt("xc%d_%d" % (g, b), [P, 512], U32, XC_OFF + 2048 * (4 * g + b))
+                    if g % 4 == 0:
+                        xs[(g // 4, b)] = sbt("xs%d_%d" % (g // 4, b), [P, 512], U8, XS_OFF + 512 * (g + b))
+                nc.vector.quantize_mx(
+                    out=xc[(g, b)][:, 128 * i4 : 128 * (i4 + 1)].bitcast(FP8X4),
+                    scales=xplane(g, b)[:, 128 * i4 : 128 * (i4 + 1)],
+                    in_=xgrp[(s, q // 4)][:, 512 * (q % 4) : 512 * (q % 4 + 1)],
+                )
 
         def xplane(g, b):
             return xs[(g // 4, b)][4 * (g % 4) : P, :]
@@ -434,38 +477,46 @@ def tile_multilatentattention_pa_l_kernel(tc, x, Wqa, Wqb, out):
             cnt["gb"] = cnt["gb"] + 1
             return sbt("gb%d" % k, [P, 2048], BF16, GB_OFF + 4096 * k)
 
+        def first_mm(g, b):
+            if g == 15:
+                sl[b] = sbt("sl%d" % b, [P, 4, 512], BF16, SL_OFF + 4096 * b)
+            for t in range(4):
+                if g == 0:
+                    acc[(b, t)] = bank(4 * (1 - b) + t)
+                mx(
+                    acc[(b, t)],
+                    w0[(g, t // 2)][0][:, 128 * (t % 2) : 128 * (t % 2 + 1)],
+                    w0[(g, t // 2)][1][:, 128 * (t % 2) : 128 * (t % 2 + 1)],
+                    xc[(g, b)],
+                    xplane(g, b),
+                    g == 0,
+                    g == 15,
+                )
+                if g == 15:
+                    copy("s" if t % 2 == 0 else "v", sl[b][:, t, :], acc[(b, t)])
+
         make_ident()
-        for n in range(5):
-            load_half()
+        for s in range(4):
+            load_a(s)
         for s in range(16):
-            transposes(s)
+            transposes_a(s)
+            if s + 4 < 16:
+                load_a(s + 4)
+            if s == 11:
+                for g in range(16):
+                    w0s_stream["items"][2 * g]["dma"]()
             if s >= 1:
-                quant_x(s - 1)
-            copy_out(s)
-        quant_x(15)
+                quant_a(s - 1)
+            copy_out_a(s)
+        quant_a(15)
         for g in range(16):
             advance(w0s_stream, 2 * (g + W0_LEAD) + 1)
             if g in (5, 7, 9, 11, 13):
                 load_half()
             if g == 12:
                 sort_x(16)
-            for b in (1, 0) if g == 15 else (0, 1):
-                if g == 15:
-                    sl[b] = sbt("sl%d" % b, [P, 4, 512], BF16, SL_OFF + 4096 * b)
-                for t in range(4):
-                    if g == 0:
-                        acc[(b, t)] = bank(4 * (1 - b) + t)
-                    mx(
-                        acc[(b, t)],
-                        w0[(g, t // 2)][0][:, 128 * (t % 2) : 128 * (t % 2 + 1)],
-                        w0[(g, t // 2)][1][:, 128 * (t % 2) : 128 * (t % 2 + 1)],
-                        xc[(g, b)],
-                        xplane(g, b),
-                        g == 0,
-                        g == 15,
-                    )
-                    if g == 15:
-                        copy("s" if t % 2 == 0 else "v", sl[b][:, t, :], acc[(b, t)])
+            for b in (0, 1) if g < HELD_FROM else (1,):
+                first_mm(g, b)
         for s in range(16, 32):
             transposes(s)
             if s >= 17:
@@ -478,7 +529,9 @@ def tile_multilatentattention_pa_l_kernel(tc, x, Wqa, Wqb, out):
             if s == 29:
                 prefetch(ws, 3)
                 ws["ahead"] = 4
-            if s >= 19:
+            if s < 19:
+                first_mm(s - 16 + HELD_FROM, 0)
+            else:
                 mm_x(s - 3)
         quant_x(31)
         advance(ws, 4)

@@ -90,8 +90,9 @@ def tile_multilatentattention_pa_l_kernel(tc, x, Wqa, Wqb, out):
                 stop=stop,
             )
 
-        cnt = {"gb": 0, "ot": 0, "tt": 0, "load": 32}
+        cnt = {"gb": 0, "ot": 0, "tt": 0, "load": 32, "pair": 0}
         xraw = {}
+        xpair = {}
         xsort = {}
         xgrp = {}
         tpb = {}
@@ -324,6 +325,35 @@ def tile_multilatentattention_pa_l_kernel(tc, x, Wqa, Wqb, out):
             )
             xraw[s].append(t.rearrange("r i k -> r (i k)").bitcast(F32))
 
+        def load_pair():
+            n = cnt["pair"]
+            cnt["pair"] = n + 1
+            if n >= 16:
+                return
+            d, half = divmod(n, 2)
+            b, dq = divmod(d, 4)
+            row = 512 * b + 256 * half
+            off = U_OFF + 8192 * (n % 4)
+            if d == 0:
+                return
+            t = sbt("xp%d" % (n % 4), [P, 2, 2048], BF16, off)
+            nc.sync.dma_start(
+                out=t, in_=x2[row : row + 256, 2048 * dq : 2048 * (dq + 1)].rearrange("(i r) k -> r i k", r=P)
+            )
+            xpair[n] = t.rearrange("r i k -> r (i k)").bitcast(F32)
+
+        def load_first():
+            for r in range(2):
+                for half in range(2):
+                    t = sbt("xfirst%d" % (2 * r + half), [P, 2, 1024], BF16, U_OFF + 8192 * half + 4096 * r)
+                    nc.sync.dma_start(
+                        out=t,
+                        in_=x2[256 * half : 256 * (half + 1), 1024 * r : 1024 * (r + 1)].rearrange(
+                            "(i r) k -> r i k", r=P
+                        ),
+                    )
+                    xpair[(r, half)] = t.rearrange("r i k -> r (i k)").bitcast(F32)
+
         def sort_x(s):
             xsort[s] = []
             for half in range(2):
@@ -336,8 +366,15 @@ def tile_multilatentattention_pa_l_kernel(tc, x, Wqa, Wqb, out):
                 load_half()
 
         def x_words(s, ih, il, gl, u):
-            lo = 256 * (2 * il + gl) + 128 * u
-            return xsort[s][ih][:, lo : lo + 128]
+            if s >= SORT_FROM:
+                lo = 256 * (2 * il + gl) + 128 * u
+                return xsort[s][ih][:, lo : lo + 128]
+            d, r = divmod(s, 2)
+            if d == 0:
+                lo = 512 * il + 256 * gl
+                return xpair[(r, ih)][:, lo + u : lo + 256 : 2]
+            lo = 1024 * il + 256 * (2 * r + gl)
+            return xpair[2 * d + ih][:, lo + u : lo + 256 : 2]
 
         def transposes(s):
             for ih in range(2):
@@ -352,6 +389,11 @@ def tile_multilatentattention_pa_l_kernel(tc, x, Wqa, Wqb, out):
                                 in_=x_words(s, ih, il, gl, u),
                                 identity=tab["ident"],
                             )
+                if s < SORT_FROM and s % 2 == 1:
+                    load_pair()
+                    if cnt["pair"] == 16:
+                        for g in range(16):
+                            w0s_stream["items"][2 * g]["dma"]()
 
         def copy_out(s):
             for gl in range(2):
@@ -361,68 +403,10 @@ def tile_multilatentattention_pa_l_kernel(tc, x, Wqa, Wqb, out):
             for ih in range(2):
                 for gl in range(2):
                     copy(
-                        "s",
+                        "v" if (s < SORT_FROM and gl == 0 and ih == 0) else "s",
                         xgrp[(s, gl)].bitcast(F32)[:, 512 * ih : 512 * (ih + 1)].rearrange("p (r u) -> p r u", u=2),
                         tpb[(s, gl, ih)].rearrange("p u r -> p r u"),
                     )
-
-        def load_a(s):
-            b, rest = divmod(s, 8)
-            kh, i4 = divmod(rest, 4)
-            row = 512 * b + 128 * i4
-            off = U_OFF + 8192 * (s % 4)
-            if s == 0:
-                xraw[s] = []
-                for j in range(4):
-                    t = sbt("xfirst%d" % j, [P, 1024], BF16, off + 2048 * j)
-                    nc.sync.dma_start(out=t, in_=x2[row : row + 128, 1024 * j : 1024 * (j + 1)])
-                    xraw[s].append(t.bitcast(F32))
-            else:
-                t = sbt("xa%d" % (s % 4), [P, 4096], BF16, off)
-                nc.sync.dma_start(out=t, in_=x2[row : row + 128, 4096 * kh : 4096 * (kh + 1)])
-                words = t.bitcast(F32)
-                xraw[s] = [words[:, 512 * j : 512 * (j + 1)] for j in range(4)]
-
-        def transposes_a(s):
-            for j in range(4):
-                tp = bank(j).rearrange("p (g u r) -> p g u r", g=2, u=2)
-                tpb[(s, j)] = tp
-                for gl in range(2):
-                    for u in range(2):
-                        nc.tensor.transpose(
-                            out=tp[:, gl, u, :],
-                            in_=xraw[s][j][:, 256 * gl + u : 256 * (gl + 1) : 2],
-                            identity=tab["ident"],
-                        )
-
-        def copy_out_a(s):
-            for jj in range(2):
-                k = cnt["gb"] % 3
-                cnt["gb"] = cnt["gb"] + 1
-                xgrp[(s, jj)] = sbt("gb%d" % k, [P, 2048], BF16, GB_OFF + 4096 * k)
-                for jl in range(2):
-                    copy(
-                        "v" if (jj == 0 and jl == 0) else "s",
-                        xgrp[(s, jj)].bitcast(F32)[:, 512 * jl : 512 * (jl + 1)].rearrange(
-                            "p (g r u) -> p g r u", g=2, u=2
-                        ),
-                        tpb[(s, 2 * jj + jl)].rearrange("p g u r -> p g r u"),
-                    )
-
-        def quant_a(s):
-            b, rest = divmod(s, 8)
-            kh, i4 = divmod(rest, 4)
-            for q in range(8):
-                g = 8 * kh + q
-                if i4 == 0:
-                    xc[(g, b)] = sbt("xc%d_%d" % (g, b), [P, 512], U32, XC_OFF + 2048 * (4 * g + b))
-                    if g % 4 == 0:
-                        xs[(g // 4, b)] = sbt("xs%d_%d" % (g // 4, b), [P, 512], U8, XS_OFF + 512 * (g + b))
-                nc.vector.quantize_mx(
-                    out=xc[(g, b)][:, 128 * i4 : 128 * (i4 + 1)].bitcast(FP8X4),
-                    scales=xplane(g, b)[:, 128 * i4 : 128 * (i4 + 1)],
-                    in_=xgrp[(s, q // 4)][:, 512 * (q % 4) : 512 * (q % 4 + 1)],
-                )
 
         def xplane(g, b):
             return xs[(g // 4, b)][4 * (g % 4) : P, :]
@@ -496,19 +480,15 @@ def tile_multilatentattention_pa_l_kernel(tc, x, Wqa, Wqb, out):
                     copy("s" if t % 2 == 0 else "v", sl[b][:, t, :], acc[(b, t)])
 
         make_ident()
-        for s in range(4):
-            load_a(s)
+        load_first()
+        for n in range(4):
+            load_pair()
         for s in range(16):
-            transposes_a(s)
-            if s + 4 < 16:
-                load_a(s + 4)
-            if s == 11:
-                for g in range(16):
-                    w0s_stream["items"][2 * g]["dma"]()
+            transposes(s)
             if s >= 1:
-                quant_a(s - 1)
-            copy_out_a(s)
-        quant_a(15)
+                quant_x(s - 1)
+            copy_out(s)
+        quant_x(15)
         for g in range(16):
             advance(w0s_stream, 2 * (g + W0_LEAD) + 1)
             if g in (5, 7, 9, 11, 13):
@@ -628,7 +608,7 @@ def tile_multilatentattention_pa_l_kernel(tc, x, Wqa, Wqb, out):
                 g2 == 3,
             )
 
-        def finish(grp, i, bn, br, last):
+        def finish(grp, i, bn, br, late):
             a = i % 4
             tb = tab["tb"]
             k = cnt["ot"] % 6
@@ -655,7 +635,7 @@ def tile_multilatentattention_pa_l_kernel(tc, x, Wqa, Wqb, out):
                 in1=tb[:, 0, a, :].unsqueeze(1).to_broadcast([P, 4, 64]),
                 op=ALU.mult,
             )
-            adder = nc.vector if last else nc.gpsimd
+            adder = nc.vector if late else nc.gpsimd
             adder.tensor_tensor(
                 out=ot[:, :, 128:256].rearrange("p h (j e) -> p h j e", e=2),
                 in0=t1,
@@ -663,14 +643,7 @@ def tile_multilatentattention_pa_l_kernel(tc, x, Wqa, Wqb, out):
                 op=ALU.add,
             )
             rows = out2[128 * i : 128 * (i + 1), 1024 * grp : 1024 * (grp + 1)]
-            if last:
-                for half in (1, 0):
-                    nc.sync.dma_start(
-                        out=rows.rearrange("p (h d) -> p h d", h=4)[:, :, 128 * half : 128 * (half + 1)],
-                        in_=ot[:, :, 128 * half : 128 * (half + 1)],
-                    )
-            else:
-                nc.sync.dma_start(out=rows, in_=ot.rearrange("p h d -> p (h d)"))
+            nc.sync.dma_start(out=rows, in_=ot.rearrange("p h d -> p (h d)"))
 
         pre = {}
         for i in range(4):
@@ -691,4 +664,4 @@ def tile_multilatentattention_pa_l_kernel(tc, x, Wqa, Wqb, out):
             for kind in (1, 0) if it == 63 else (0, 1):
                 for g2 in range(4):
                     s2_mm(grp, i, kind, br if kind == 1 else bn, g2)
-            finish(grp, i, bn, br, it == 63)
+            finish(grp, i, bn, br, it >= 61)

from contextlib import ExitStack
import math

import concourse.masks as masks
import concourse.mybir as mybir

F32 = mybir.dt.float32
BF16 = mybir.dt.bfloat16
U32 = mybir.dt.uint32
U8 = mybir.dt.uint8
I32 = mybir.dt.int32
FP8X4 = mybir.dt.float8_e4m3fn_x4
ALU = mybir.AluOpType
ACTF = mybir.ActivationFunctionType

FLOPS = 2 * 2048 * 8192 * 2048 + 2 * 2048 * 2048 * 4096

P = 128
ROPE_BASE = 10000.0

XC_OFF = 0
XS_OFF = 131072
U_OFF = 139264
RAW_OFF = U_OFF
XH_OFF = (U_OFF + 8192, U_OFF + 12288, U_OFF + 16384, U_OFF + 20480, U_OFF)
SO_OFF = U_OFF + 24576
SORT_FROM = 16
WQ0_OFF = U_OFF + 16384
GB_OFF = U_OFF + 32768
CQ_OFF = U_OFF + 40960
CQS_OFF = CQ_OFF + 24576
WQ0S_OFF = CQS_OFF + 2048
W0C_OFF = U_OFF + 45056
ID_OFF = U_OFF + 67584
W0S_OFF = U_OFF + 68096
P_OFF = U_OFF + 68608
WG_OFF = P_OFF
RC_OFF = P_OFF + 4096
RS_OFF = P_OFF + 10240
CQ3_OFF = P_OFF
CQ3S_OFF = P_OFF + 8192
SL_OFF = P_OFF + 11776
TB_OFF = SL_OFF + 16384
EXT_OFF = TB_OFF + 3072
QR_OFF = 0
QG_OFF = 32768
WQ_OFF = 40960
WQ_SIZE = 17408
OT_OFF = 93184
T1_OFF = 117760
T2_OFF = 123904

SWEEPS = ((1, 0), (1, 1), (2, 0), (2, 1), (3, 0), (3, 1))
LEAD = 4
W0_LEAD = 1
HELD_FROM = 13
RING = 6


def tile_multilatentattention_pa_l_kernel(tc, x, Wqa, Wqb, out):
    nc = tc.nc
    x2 = x.rearrange("b s d -> (b s) d")
    out2 = out.rearrange("b s h d -> (b s) (h d)")

    with ExitStack() as ctx:
        sb = ctx.enter_context(tc.tile_pool(name="sb", bufs=1))
        ps = ctx.enter_context(tc.psum_pool(name="ps", bufs=1))
        ctx.enter_context(tc.manual_schedule())

        def sbt(tag, shape, dtype, off):
            return sb.tile(shape, dtype, name=tag, tag=tag, offset=off, align_bytes=64)

        def bank(k):
            return ps.tile([P, 512], F32, name="bank%d" % k, tag="bank%d" % k)

        def copy(eng, dst, src):
            if eng == "s":
                nc.scalar.copy(out=dst, in_=src)
            else:
                nc.vector.tensor_copy(out=dst, in_=src)

        def mx(acc, wc, wsc, mc, msc, start, stop):
            nc.tensor.matmul_mx(
                out=acc,
                lhsT=wc.bitcast(FP8X4),
                lhsT_scale=wsc,
                rhs=mc.bitcast(FP8X4),
                rhs_scale=msc,
                start=start,
                stop=stop,
            )

        cnt = {"gb": 0, "ot": 0, "tt": 0, "load": 32, "pair": 0}
        xraw = {}
        xpair = {}
        xsort = {}
        xgrp = {}
        tpb = {}
        xc = {}
        xs = {}
        w0 = {}
        wraw = {}
        ring = {}
        sl = {}
        cq = {}
        cqs = {}
        cqg = {}
        wq = {}
        wqs = {}
        acc = {}
        tab = {}

        def advance(st, target):
            items = st["items"]
            last = len(items) - 1
            for k in range(st["q"], min(target, last) + 1):
                for i in range(st["i"], k + 1):
                    items[i]["inter"]()
                    st["i"] = i + 1
                items[k]["quant"]()
                st["q"] = k + 1
                for i in range(st["i"], min(k + st["look"], last) + 1):
                    items[i]["inter"]()
                    st["i"] = i + 1
                prefetch(st, st["i"] - 1 + st["ahead"])

        def prefetch(st, upto):
            items = st["items"]
            for d in range(st["d"], min(upto, len(items) - 1) + 1):
                if items[d]["dma"] is not None:
                    items[d]["dma"]()
                st["d"] = d + 1

        def w_item(c_chunk, h, g, idx, first):
            cell = {}

            def dma():
                if first:
                    rt = sbt("w0r%d" % g, [P, 4, 512], BF16, XC_OFF + 8192 * g + 4096)
                else:
                    rt = sbt("raw%d" % (idx % 4), [P, 4, 512], BF16, RAW_OFF + 4096 * (idx % 4))
                nc.sync.dma_start(
                    out=rt,
                    in_=Wqa[512 * g : 512 * (g + 1), 512 * c_chunk : 512 * (c_chunk + 1)].rearrange(
                        "(p j) c -> p j c", j=4
                    ),
                )
                wraw[(first, g if first else idx)] = rt

            def inter():
                k = idx % 4 if first else idx % 2
                wg = sbt("wg%d" % k, [P, 1024], BF16, WG_OFF + 2048 * k if k < 2 else SL_OFF + 4096 + 2048 * k)
                copy(
                    "s" if idx % 2 == 0 else "v",
                    wg.rearrange("p (t m j) -> p t m j", t=2, j=4),
                    wraw[(first, g if first else idx)].rearrange("p j (m t) -> p t m j", t=4)[:, 2 * h : 2 * h + 2],
                )
                cell["wg"] = wg

            def quant():
                if first:
                    if idx < 6:
                        off = RC_OFF + 1024 * idx
                    elif idx < 28:
                        off = W0C_OFF + 1024 * (idx - 6)
                    elif idx < 31:
                        off = TB_OFF + 1024 * (idx - 28)
                    else:
                        off = EXT_OFF
                    codes = sbt("w0c%d" % idx, [P, 256], U32, off)
                    if idx < 6:
                        off = RS_OFF + 256 * idx
                    elif idx < 22:
                        off = SL_OFF + 12288 + 256 * (idx - 6)
                    elif idx < 24:
                        off = W0S_OFF + 256 * (idx - 22)
                    else:
                        off = EXT_OFF + 1024 + 256 * (idx - 24)
                    scales = sbt("w0s%d" % idx, [P, 256], U8, off)
                    w0[(g, h)] = (codes, scales)
                else:
                    k = idx % RING
                    codes = sbt("rc%d" % k, [P, 256], U32, RC_OFF + 1024 * k)
                    scales = sbt("rs%d" % k, [P, 256], U8, RS_OFF + 256 * k)
                    ring[idx] = (codes, scales)
                nc.vector.quantize_mx(out=codes.bitcast(FP8X4), scales=scales, in_=cell["wg"])

            return {"dma": dma if (h == 0 or not first) else None, "inter": inter, "quant": quant}

        def q_load(grp, g2, hp, rt):
            nc.sync.dma_start(
                out=rt,
                in_=Wqb[
                    512 * g2 : 512 * (g2 + 1), 1024 * grp + 512 * hp : 1024 * grp + 512 * (hp + 1)
                ].rearrange("(p j) c -> p j c", j=4),
            )

        def q_inter(eng, rt, kind, gt):
            copy(
                eng,
                gt.rearrange("p (h c j) -> p h c j", h=2, j=4),
                rt.rearrange("p j (h c) -> p h c j", h=2)[:, :, 128 * kind : 128 * (kind + 1), :],
            )

        def q_quant(grp, kind, g2, hp, gt):
            base = WQ0_OFF if grp == 0 else WQ_OFF + WQ_SIZE * (grp - 1)
            sbase = WQ0S_OFF if grp == 0 else base + 16384
            if hp == 0:
                wq[(grp, kind, g2)] = sbt(
                    "wq%d_%d_%d" % (grp, kind, g2), [P, 512], U32, base + 2048 * (4 * kind + g2)
                )
                if g2 == 0:
                    wqs[(grp, kind)] = sbt("wqs%d_%d" % (grp, kind), [P, 512], U8, sbase + 512 * kind)
            nc.vector.quantize_mx(
                out=wq[(grp, kind, g2)][:, 256 * hp : 256 * (hp + 1)].bitcast(FP8X4),
                scales=wqs[(grp, kind)][4 * g2 : P, 256 * hp : 256 * (hp + 1)],
                in_=gt,
            )

        def q_item(n, shared):
            r, kind = divmod(n, 2)
            grp = 1 + r // 8
            g2, hp = divmod(r % 8, 2)
            cell = {}

            def dma():
                rt = sbt("qr%d" % (r % 8), [P, 4, 512], BF16, QR_OFF + 4096 * (r % 8))
                q_load(grp, g2, hp, rt)
                shared[r] = rt

            def inter():
                gt = sbt("qg%d" % (n % 4), [P, 1024], BF16, QG_OFF + 2048 * (n % 4))
                q_inter("v" if (n < 16 and kind == 1) else "s", shared[r], kind, gt)
                cell["gt"] = gt

            def quant():
                q_quant(grp, kind, g2, hp, cell["gt"])

            return {"dma": dma if kind == 0 else None, "inter": inter, "quant": quant}

        w0s_stream = {
            "items": [w_item(0, n % 2, n // 2, n, True) for n in range(32)],
            "d": 32,
            "i": 0,
            "q": 0,
            "ahead": 0,
            "look": 2,
        }
        ws = {
            "items": [w_item(SWEEPS[q // 16][0], SWEEPS[q // 16][1], q % 16, q, False) for q in range(96)],
            "d": 0,
            "i": 0,
            "q": 0,
            "ahead": 0,
            "look": 1,
        }
        qshared = {}
        qs = {"items": [q_item(n, qshared) for n in range(48)], "d": 0, "i": 0, "q": 0, "ahead": 14, "look": 1}

        def make_ident():
            ident = sbt("ident", [P, P], F32, ID_OFF)
            masks.make_identity(nc, ident)
            tab["ident"] = ident

        def tables_first():
            pos_i = sbt("pos_i", [P, 4], I32, WQ0_OFF)
            nc.gpsimd.iota(pos_i, pattern=[[128, 4]], base=0, channel_multiplier=1)
            pos_f = sbt("pos_f", [P, 4], F32, WQ0_OFF + 64)
            nc.vector.tensor_copy(out=pos_f, in_=pos_i)
            turns = sbt("turns", [P, 2, 4, 64], F32, WQ0_OFF + 2048)
            nc.gpsimd.tensor_scalar(
                out=turns[:, 0, :, 0], in0=pos_f, scalar1=1.0 / (2.0 * math.pi), scalar2=None, op0=ALU.mult
            )
            for w in (1, 2, 4, 8, 16, 32):
                nc.gpsimd.tensor_scalar(
                    out=turns[:, 0, :, w : 2 * w],
                    in0=turns[:, 0, :, 0:w],
                    scalar1=ROPE_BASE ** (-w / 64.0),
                    scalar2=None,
                    op0=ALU.mult,
                )
            nc.gpsimd.tensor_scalar(out=turns[:, 1], in0=turns[:, 0], scalar1=0.25, scalar2=None, op0=ALU.add)
            tab["turns"] = turns.rearrange("p s a j -> p (s a j)")

        def tables_second():
            turns = tab["turns"]
            whole_i = sbt("whole_i", [P, 512], I32, WQ0_OFF + 4096)
            nc.vector.tensor_copy(out=whole_i, in_=turns)
            whole_f = sbt("whole_f", [P, 512], F32, WQ0_OFF + 6144)
            nc.vector.tensor_copy(out=whole_f, in_=whole_i)
            fr1 = sbt("fr1", [P, 512], F32, WQ0_OFF + 8192)
            nc.vector.tensor_tensor(out=fr1, in0=turns, in1=whole_f, op=ALU.subtract)
            fr2 = sbt("fr2", [P, 512], F32, WQ0_OFF + 10240)
            nc.vector.scalar_tensor_tensor(out=fr2, in0=fr1, scalar=0.5, in1=fr1, op0=ALU.is_gt, op1=ALU.subtract)
            fr3 = sbt("fr3", [P, 512], F32, WQ0_OFF + 12288)
            nc.vector.scalar_tensor_tensor(out=fr3, in0=fr2, scalar=0.5, in1=fr2, op0=ALU.is_gt, op1=ALU.subtract)
            tab["fr3"] = fr3

        def tables_third():
            tb = sbt("tb", [P, 3, 4, 64], F32, TB_OFF)
            nc.scalar.activation(
                out=tb[:, 0:2].rearrange("p s a j -> p (s a j)"), in_=tab["fr3"], func=ACTF.Sin, scale=2.0 * math.pi
            )
            tab["tb"] = tb

        def tables_fourth():
            tb = tab["tb"]
            nc.vector.tensor_scalar(out=tb[:, 2], in0=tb[:, 0], scalar1=-1.0, scalar2=None, op0=ALU.mult)

        def load_half():
            n = cnt["load"]
            cnt["load"] = n + 1
            if n >= 64:
                return
            s, half = divmod(n, 2)
            b, rr = divmod(s, 8)
            slot = n % 5
            row = 512 * b + 256 * half
            if half == 0:
                xraw[s] = []
            t = sbt("xh%d" % slot, [P, 2, 1024], BF16, XH_OFF[slot])
            nc.sync.dma_start(
                out=t,
                in_=x2[row : row + 256, 1024 * rr : 1024 * (rr + 1)].rearrange("(i r) k -> r i k", r=P),
            )
            xraw[s].append(t.rearrange("r i k -> r (i k)").bitcast(F32))

        def load_pair():
            n = cnt["pair"]
            cnt["pair"] = n + 1
            if n >= 16:
                return
            d, half = divmod(n, 2)
            b, dq = divmod(d, 4)
            row = 512 * b + 256 * half
            off = U_OFF + 8192 * (n % 4)
            if d == 0:
                return
            t = sbt("xp%d" % (n % 4), [P, 2, 2048], BF16, off)
            nc.sync.dma_start(
                out=t, in_=x2[row : row + 256, 2048 * dq : 2048 * (dq + 1)].rearrange("(i r) k -> r i k", r=P)
            )
            xpair[n] = t.rearrange("r i k -> r (i k)").bitcast(F32)

        def load_first():
            for r in range(2):
                for half in range(2):
                    t = sbt("xfirst%d" % (2 * r + half), [P, 2, 1024], BF16, U_OFF + 8192 * half + 4096 * r)
                    nc.sync.dma_start(
                        out=t,
                        in_=x2[256 * half : 256 * (half + 1), 1024 * r : 1024 * (r + 1)].rearrange(
                            "(i r) k -> r i k", r=P
                        ),
                    )
                    xpair[(r, half)] = t.rearrange("r i k -> r (i k)").bitcast(F32)

        def sort_x(s):
            xsort[s] = []
            for half in range(2):
                so = sbt("so%d" % half, [P, 1024], F32, SO_OFF + 4096 * half)
                nc.vector.tensor_copy(
                    out=so.rearrange("p (a u w) -> p a u w", a=4, u=2),
                    in_=xraw[s][half].rearrange("p (a w u) -> p a u w", a=4, u=2),
                )
                xsort[s].append(so)
                load_half()

        def x_words(s, ih, il, gl, u):
            if s >= SORT_FROM:
                lo = 256 * (2 * il + gl) + 128 * u
                return xsort[s][ih][:, lo : lo + 128]
            d, r = divmod(s, 2)
            if d == 0:
                lo = 512 * il + 256 * gl
                return xpair[(r, ih)][:, lo + u : lo + 256 : 2]
            lo = 1024 * il + 256 * (2 * r + gl)
            return xpair[2 * d + ih][:, lo + u : lo + 256 : 2]

        def transposes(s):
            for ih in range(2):
                for gl in range(2):
                    bk = bank(2 * ih + gl)
                    tp = bk.rearrange("p (u r) -> p u r", u=2)
                    tpb[(s, gl, ih)] = tp
                    for il in range(2):
                        for u in range(2):
                            nc.tensor.transpose(
                                out=tp[:, u, 128 * il : 128 * (il + 1)],
                                in_=x_words(s, ih, il, gl, u),
                                identity=tab["ident"],
                            )
                if s < SORT_FROM and s % 2 == 1:
                    load_pair()
                    if cnt["pair"] == 16:
                        for g in range(16):
                            w0s_stream["items"][2 * g]["dma"]()

        def copy_out(s):
            for gl in range(2):
                k = cnt["gb"] % 3
                cnt["gb"] = cnt["gb"] + 1
                xgrp[(s, gl)] = sbt("gb%d" % k, [P, 2048], BF16, GB_OFF + 4096 * k)
            for ih in range(2):
                for gl in range(2):
                    copy(
                        "v" if (s < SORT_FROM and gl == 0 and ih == 0) else "s",
                        xgrp[(s, gl)].bitcast(F32)[:, 512 * ih : 512 * (ih + 1)].rearrange("p (r u) -> p r u", u=2),
                        tpb[(s, gl, ih)].rearrange("p u r -> p r u"),
                    )

        def xplane(g, b):
            return xs[(g // 4, b)][4 * (g % 4) : P, :]

        def quant_x(s):
            b, rr = divmod(s, 8)
            for gl in range(2):
                g = 2 * rr + gl
                xc[(g, b)] = sbt("xc%d_%d" % (g, b), [P, 512], U32, XC_OFF + 2048 * (4 * g + b))
                if g % 4 == 0:
                    xs[(g // 4, b)] = sbt("xs%d_%d" % (g // 4, b), [P, 512], U8, XS_OFF + 512 * (g + b))
                nc.vector.quantize_mx(out=xc[(g, b)].bitcast(FP8X4), scales=xplane(g, b), in_=xgrp[(s, gl)])

        def mm_x(s):
            b, rr = divmod(s, 8)
            for gl in range(2):
                g = 2 * rr + gl
                for t in range(4):
                    if g == 0:
                        acc[(b, t)] = bank(4 + t)
                    mx(
                        acc[(b, t)],
                        w0[(g, t // 2)][0][:, 128 * (t % 2) : 128 * (t % 2 + 1)],
                        w0[(g, t // 2)][1][:, 128 * (t % 2) : 128 * (t % 2 + 1)],
                        xc[(g, b)],
                        xplane(g, b),
                        g == 0,
                        g == 15,
                    )
            if rr == 7:
                sl[b] = sbt("sl%d" % b, [P, 4, 512], BF16, SL_OFF + 4096 * b)
                for t in range(4):
                    copy("s" if t % 2 == 0 else "v", sl[b][:, t, :], acc[(b, t)])

        def cq_inter(eng, b, gt):
            copy(eng, gt.rearrange("p (n t) -> p n t", t=4), sl[b].rearrange("p t n -> p n t"))
            cqg[b] = gt

        def cq_quant(c_chunk, b):
            if c_chunk < 3:
                cq[(c_chunk, b)] = sbt("cq%d_%d" % (c_chunk, b), [P, 512], U32, CQ_OFF + 2048 * (4 * c_chunk + b))
                if c_chunk == 0:
                    tab[("cqsa", b)] = sbt("cqsa%d" % b, [P, 512], U8, CQS_OFF + 512 * b)
                cqs[(c_chunk, b)] = tab[("cqsa", b)][4 * c_chunk : P, :]
            else:
                cq[(c_chunk, b)] = sbt("cq3_%d" % b, [P, 512], U32, CQ3_OFF + 2048 * b)
                cqs[(c_chunk, b)] = sbt("cqsb%d" % b, [P, 512], U8, CQ3S_OFF + 512 * b)
            nc.vector.quantize_mx(out=cq[(c_chunk, b)].bitcast(FP8X4), scales=cqs[(c_chunk, b)], in_=cqg[b])

        def gb_tile():
            k = cnt["gb"] % 2
            cnt["gb"] = cnt["gb"] + 1
            return sbt("gb%d" % k, [P, 2048], BF16, GB_OFF + 4096 * k)

        def first_mm(g, b):
            if g == 15:
                sl[b] = sbt("sl%d" % b, [P, 4, 512], BF16, SL_OFF + 4096 * b)
            for t in range(4):
                if g == 0:
                    acc[(b, t)] = bank(4 * (1 - b) + t)
                mx(
                    acc[(b, t)],
                    w0[(g, t // 2)][0][:, 128 * (t % 2) : 128 * (t % 2 + 1)],
                    w0[(g, t // 2)][1][:, 128 * (t % 2) : 128 * (t % 2 + 1)],
                    xc[(g, b)],
                    xplane(g, b),
                    g == 0,
                    g == 15,
                )
                if g == 15:
                    copy("s" if t % 2 == 0 else "v", sl[b][:, t, :], acc[(b, t)])

        make_ident()
        load_first()
        for n in range(4):
            load_pair()
        for s in range(16):
            transposes(s)
            if s >= 1:
                quant_x(s - 1)
            copy_out(s)
        quant_x(15)
        for g in range(16):
            advance(w0s_stream, 2 * (g + W0_LEAD) + 1)
            if g in (5, 7, 9, 11, 13):
                load_half()
            if g == 12:
                sort_x(16)
            for b in (0, 1) if g < HELD_FROM else (1,):
                first_mm(g, b)
        for s in range(16, 32):
            transposes(s)
            if s >= 17:
                quant_x(s - 1)
            if s + 1 < 32:
                sort_x(s + 1)
            copy_out(s)
            if s == 28:
                prefetch(ws, 1)
            if s == 29:
                prefetch(ws, 3)
                ws["ahead"] = 4
            if s < 19:
                first_mm(s - 16 + HELD_FROM, 0)
            else:
                mm_x(s - 3)
        quant_x(31)
        advance(ws, 4)
        mm_x(29)
        mm_x(30)
        mm_x(31)

        cnt["gb"] = 0
        q0 = {}

        def side_work(sw, g):
            if sw in (0, 2, 4) and 3 <= g <= 10:
                b, ph = divmod(g - 3, 2)
                if ph == 0:
                    cq_inter("v" if b % 2 == 0 else "s", b, gb_tile())
                else:
                    cq_quant(sw // 2, b)
            if sw == 0:
                if g == 1:
                    tables_first()
                if g == 11:
                    tables_second()
                if g == 13:
                    tables_third()
                if g == 14:
                    tables_fourth()
            for j in range(2):
                for k in range(4):
                    g2, hp = divmod(4 * j + k, 2)
                    if (sw, g) == (2 * j + 1, 4 * k):
                        q0["raw"] = sbt("q0raw", [P, 4, 512], BF16, GB_OFF)
                        q_load(0, g2, hp, q0["raw"])
                    if (sw, g) == ((2 * j + 1, 4 * k + 3) if k < 3 else (2 * j + 2, 0)):
                        for kind in range(2):
                            q0[kind] = sbt("q0g%d" % kind, [P, 1024], BF16, GB_OFF + 4096 + 2048 * kind)
                            q_inter("s" if kind == 0 else "v", q0["raw"], kind, q0[kind])
                    if (sw, g) == ((2 * j + 1, 4 * k + 4) if k < 3 else (2 * j + 2, 2)):
                        for kind in range(2):
                            q_quant(0, kind, g2, hp, q0[kind])
            if sw == 5:
                if g >= 8:
                    prefetch(qs, min(15, 4 * (g - 7) - 1))
                if g >= 11:
                    advance(qs, 2 * (g - 11) + 1)

        def sweep_mm(sw, g, b):
            h = SWEEPS[sw][1]
            q = 16 * sw + g
            for tau in range(2):
                if g == 0:
                    acc[(b, tau)] = bank(2 * b + tau)
                mx(
                    acc[(b, tau)],
                    ring[q][0][:, 128 * tau : 128 * (tau + 1)],
                    ring[q][1][:, 128 * tau : 128 * (tau + 1)],
                    xc[(g, b)],
                    xplane(g, b),
                    g == 0,
                    g == 15,
                )
                if g == 15:
                    if h == 0 and tau == 0:
                        sl[b] = sbt("sl%d" % b, [P, 4, 512], BF16, SL_OFF + 4096 * b)
                    copy("s" if tau == 0 else "v", sl[b][:, 2 * h + tau, :], acc[(b, tau)])

        for sw in range(6):
            for g in range(16):
                advance(ws, 16 * sw + g + LEAD)
                side_work(sw, g)
                for b in range(4):
                    sweep_mm(sw, g, b)

        def g3(b):
            return sbt("g3_%d" % b, [P, 2048], BF16, OT_OFF + 4096 * b)

        cq_inter("v", 0, g3(0))
        cq_inter("s", 1, g3(1))
        cq_quant(3, 0)
        cq_inter("v", 2, g3(2))
        cq_quant(3, 1)
        cq_inter("s", 3, g3(3))
        cq_quant(3, 2)
        cq_quant(3, 3)

        def s2_mm(grp, i, kind, bk, g2):
            b, i4 = divmod(i, 4)
            mx(
                bk,
                cq[(g2, b)][:, 128 * i4 : 128 * (i4 + 1)],
                cqs[(g2, b)][:, 128 * i4 : 128 * (i4 + 1)],
                wq[(grp, kind, g2)],
                wqs[(grp, kind)][4 * g2 : P, :],
                g2 == 0,
                g2 == 3,
            )

        def finish(grp, i, bn, br, late):
            a = i % 4
            tb = tab["tb"]
            k = cnt["ot"] % 6
            cnt["ot"] = cnt["ot"] + 1
            ot = sbt("ot%d" % k, [P, 4, 256], F32, OT_OFF + 4096 * k)
            nc.scalar.copy(out=ot[:, :, 0:128], in_=bn.rearrange("p (h d) -> p h d", h=4))
            k = cnt["tt"] % 3
            cnt["tt"] = cnt["tt"] + 1
            pr = br.rearrange("p (h j e) -> p h j e", h=4, e=2)
            t1 = sbt("t1_%d" % k, [P, 4, 64, 2], F32, T1_OFF + 2048 * k)
            t2 = sbt("t2_%d" % k, [P, 4, 2, 64], F32, T2_OFF + 2048 * k)
            nc.vector.tensor_tensor(
                out=t1, in0=pr, in1=tb[:, 1, a, :].unsqueeze(1).unsqueeze(3).to_broadcast([P, 4, 64, 2]), op=ALU.mult
            )
            nc.vector.tensor_tensor(
                out=t2[:, :, 0, :],
                in0=pr[:, :, :, 1],
                in1=tb[:, 2, a, :].unsqueeze(1).to_broadcast([P, 4, 64]),
                op=ALU.mult,
            )
            nc.vector.tensor_tensor(
                out=t2[:, :, 1, :],
                in0=pr[:, :, :, 0],
                in1=tb[:, 0, a, :].unsqueeze(1).to_broadcast([P, 4, 64]),
                op=ALU.mult,
            )
            adder = nc.vector if late else nc.gpsimd
            adder.tensor_tensor(
                out=ot[:, :, 128:256].rearrange("p h (j e) -> p h j e", e=2),
                in0=t1,
                in1=t2.rearrange("p h e j -> p h j e"),
                op=ALU.add,
            )
            rows = out2[128 * i : 128 * (i + 1), 1024 * grp : 1024 * (grp + 1)]
            nc.sync.dma_start(out=rows, in_=ot.rearrange("p h d -> p (h d)"))

        pre = {}
        for i in range(4):
            for kind in range(2):
                pre[(i, kind)] = bank(2 * i + kind)
                for g2 in range(3):
                    s2_mm(0, i, kind, pre[(i, kind)], g2)
        for i in range(4):
            advance(qs, 10 + i)
            for kind in range(2):
                s2_mm(0, i, kind, pre[(i, kind)], 3)
            finish(0, i, pre[(i, 0)], pre[(i, 1)], False)
        for it in range(4, 64):
            grp, i = divmod(it, 16)
            advance(qs, 10 + (7 * it) // 8 if it > 8 else 10 + it)
            bn = bank((2 * i) % 8)
            br = bank((2 * i + 1) % 8)
            for kind in (1, 0) if it == 63 else (0, 1):
                for g2 in range(4):
                    s2_mm(grp, i, kind, br if kind == 1 else bn, g2)
            finish(grp, i, bn, br, it >= 61)
